import numpy as np
import ml_dtypes


def mxq(x, axis, fmt="e4m3"):
    dtype, down = {"e4m3": (ml_dtypes.float8_e4m3fn, 7), "e5m2": (ml_dtypes.float8_e5m2, 14)}[fmt]
    v = np.moveaxis(np.asarray(x, np.float32).astype(ml_dtypes.bfloat16).astype(np.float64), axis, -1)
    blocks = v.reshape(v.shape[:-1] + (-1, 32))
    amax = np.abs(blocks).max(-1, keepdims=True)
    byte = np.maximum(np.where(amax > 0, np.frexp(amax)[1] - 1 + 127, 0) - down, 1)
    scale = np.exp2(byte - 127.0)
    codes = (blocks / scale).astype(np.float32).astype(dtype).astype(np.float64)
    return np.moveaxis((codes * scale).reshape(v.shape), -1, axis)


WIDE = False


def mx_kscale(k):
    if not WIDE:
        return np.ones(k)
    levels = np.array([10, -10, 5, -5, 0])
    a = np.random.permutation(np.resize(levels, k // 512 * 4)).reshape(k // 512, 4)
    idx = np.arange(k)
    return np.exp2(a[idx // 512, idx % 128 // 32])


BF16 = ml_dtypes.bfloat16


def bf(x):
    return np.asarray(x, np.float32).astype(BF16)


def f64(x):
    return np.asarray(x).astype(np.float64)


B, IN, OUT, G, SH = 1024, 1024, 1024, 3, 512
LN_EPS = 1e-5


def sigmoid(v):
    return 1.0 / (1.0 + np.exp(-v))


def setup_inputs():
    t = mx_kscale(SH)
    return {"kan_sum": bf(np.random.standard_normal((B, OUT)) * 0.9 + 0.3 * np.random.standard_normal((B, 1))),
            "ln_gamma": bf(1.0 + 0.1 * np.random.standard_normal(OUT)),
            "ln_beta": bf(0.1 * np.random.standard_normal(OUT)),
            "se_w1": bf(np.random.standard_normal((SH, OUT)) / np.sqrt(OUT) * t[:, None]),
            "se_b1": bf(0.2 * np.random.standard_normal(SH) * t),
            "se_w2": bf(np.random.standard_normal((OUT, SH)) * 1.5 / np.sqrt(SH) / t[None, :]),
            "se_b2": bf(0.2 * np.random.standard_normal(OUT))}


def reference(kan_sum, ln_gamma, ln_beta, se_w1, se_b1, se_w2, se_b2):
    z = f64(kan_sum)
    mu = z.mean(axis=-1, keepdims=True)
    var = ((z - mu) ** 2).mean(axis=-1, keepdims=True)
    y = (z - mu) / np.sqrt(var + LN_EPS) * f64(ln_gamma) + f64(ln_beta)
    h = np.maximum((mxq(y, 1, "e4m3") @ mxq(f64(se_w1), 1, "e4m3").T) + f64(se_b1), 0.0)
    gate = sigmoid((mxq(h, 1, "e4m3") @ mxq(f64(se_w2), 1, "e4m3").T) + f64(se_b2))
    return y * gate

@@ -1,0 +1,211 @@
+import concourse.mybir as mybir
+from concourse.masks import make_identity
+
+F32 = mybir.dt.float32
+BF16 = mybir.dt.bfloat16
+U32 = mybir.dt.uint32
+U8 = mybir.dt.uint8
+FP8X4 = mybir.dt.float8_e4m3fn_x4
+ALU = mybir.AluOpType
+ACT = mybir.ActivationFunctionType
+
+P = 128
+PACK = 4
+K_PASS = P * PACK
+N_MAX = 512
+
+ROWS, FEAT, HID = 1024, 1024, 512
+LN_EPS = 1e-5
+ROW_TILES = ROWS // P
+FEAT_TILES = FEAT // P
+HID_TILES = HID // P
+FEAT_PASSES = FEAT // K_PASS
+ROUNDS = ROWS // N_MAX
+TILES_PER_ROUND = N_MAX // P
+
+FLOPS = 2 * ROWS * FEAT * HID * 2
+
+
+def tile_kanlayer_pb_kernel(tc, kan_sum, ln_gamma, ln_beta, se_w1, se_b1, se_w2, se_b2, out):
+    nc = tc.nc
+    with tc.tile_pool(name="keep", bufs=1) as keep, tc.tile_pool(name="small", bufs=4) as small, tc.tile_pool(
+        name="work", bufs=2
+    ) as work, tc.psum_pool(name="flip", bufs=4) as flip, tc.psum_pool(name="sums", bufs=4) as sums:
+        z_all = keep.tile([P, ROW_TILES, FEAT], BF16)
+        w1_raw = keep.tile([P, HID_TILES, FEAT], BF16)
+        w2_raw = keep.tile([P, FEAT_TILES, HID], BF16)
+        for i in range(TILES_PER_ROUND):
+            nc.sync.dma_start(out=z_all[:, i, :], in_=kan_sum[i * P : (i + 1) * P, :])
+        nc.sync.dma_start(out=w1_raw[:], in_=se_w1.rearrange("(m p) f -> p m f", p=P))
+        for i in range(TILES_PER_ROUND, ROW_TILES):
+            nc.sync.dma_start(out=z_all[:, i, :], in_=kan_sum[i * P : (i + 1) * P, :])
+        nc.sync.dma_start(out=w2_raw[:], in_=se_w2.rearrange("(j p) h -> p j h", p=P))
+
+        gamma_bc = keep.tile([P, FEAT], BF16)
+        beta_bc = keep.tile([P, FEAT], BF16)
+        nc.scalar.dma_start(out=gamma_bc[:], in_=ln_gamma.partition_broadcast(P))
+        nc.scalar.dma_start(out=beta_bc[:], in_=ln_beta.partition_broadcast(P))
+        bias_rows = keep.tile([P, P], BF16)
+        nc.vector.memset(bias_rows[:], 0.0)
+        nc.scalar.dma_start(out=bias_rows[0:HID_TILES, :], in_=se_b1.rearrange("(m p) -> m p", p=P))
+        nc.scalar.dma_start(
+            out=bias_rows[HID_TILES : HID_TILES + FEAT_TILES, :], in_=se_b2.rearrange("(j p) -> j p", p=P)
+        )
+
+        ident_bf16 = keep.tile([P, P], BF16)
+        make_identity(nc, ident_bf16[:])
+        ident_f32 = keep.tile([P, P], F32)
+        make_identity(nc, ident_f32[:])
+        minus_half = keep.tile([P, 1], F32)
+        nc.gpsimd.memset(minus_half[:], -0.5)
+
+        bias_flip = flip.tile([P, P], BF16, tag="flip")
+        nc.tensor.transpose(bias_flip[:], bias_rows[:], ident_bf16[:])
+        bias_cols = keep.tile([P, HID_TILES + FEAT_TILES], F32)
+        nc.vector.tensor_copy(out=bias_cols[:], in_=bias_flip[:, 0 : HID_TILES + FEAT_TILES])
+
+        w1_codes = keep.tile([P, FEAT_PASSES, HID], U32, align_bytes=64)
+        w1_scales = keep.tile([P, FEAT_PASSES, HID], U8, align_bytes=64)
+        w2_codes = keep.tile([P, FEAT], U32, align_bytes=64)
+        w2_scales = keep.tile([P, FEAT], U8, align_bytes=64)
+        y_codes = keep.tile([P, FEAT_PASSES, ROWS], U32, align_bytes=64)
+        y_scales = keep.tile([P, FEAT_PASSES, ROWS], U8, align_bytes=64)
+        h_codes = keep.tile([P, ROWS], U32, align_bytes=64)
+        h_scales = keep.tile([P, ROWS], U8, align_bytes=64)
+        y_all = keep.tile([P, ROW_TILES, FEAT], F32)
+
+        def flip_512_of_k(src, ident, dtype, grouped):
+            flipped = flip.tile([P, PACK, P], dtype, tag="flip")
+            for t in range(PACK):
+                nc.tensor.transpose(flipped[:, t, :], src[:, t * P : (t + 1) * P], ident)
+            nc.scalar.copy(out=grouped, in_=flipped[:].rearrange("p t r -> p r t"))
+
+        w1_grouped = keep.tile([P, FEAT_PASSES, HID, PACK], BF16, align_bytes=64)
+        for c in range(FEAT_PASSES):
+            for m in range(HID_TILES):
+                flip_512_of_k(
+                    w1_raw[:, m, c * K_PASS : (c + 1) * K_PASS],
+                    ident_bf16[:],
+                    BF16,
+                    w1_grouped[:, c, m * P : (m + 1) * P, :],
+                )
+            nc.vector.quantize_mx(
+                out=w1_codes[:, c, :].bitcast(FP8X4),
+                scales=w1_scales[:, c, :],
+                in_=w1_grouped[:, c, :, :].rearrange("p r t -> p (r t)"),
+            )
+
+        def layer_norm(i):
+            z = z_all[:, i, :]
+            stats = small.tile([P, FEAT // N_MAX, 6], F32)
+            for s in range(FEAT // N_MAX):
+                nc.vector.bn_stats(out=stats[:, s, :], in_=z[:, s * N_MAX : (s + 1) * N_MAX])
+            mean_var = small.tile([P, 2], F32)
+            nc.vector.bn_aggr(out=mean_var[:], in_=stats[:].rearrange("p s d -> p (s d)"))
+            var_eps = small.tile([P, 1], F32)
+            nc.gpsimd.tensor_scalar(
+                out=var_eps[:], in0=mean_var[:, 1:2], scalar1=1.0, scalar2=LN_EPS, op0=ALU.mult, op1=ALU.add
+            )
+            rstd = small.tile([P, 1], F32)
+            nc.gpsimd.tensor_tensor(out=rstd[:], in0=var_eps[:], in1=minus_half[:], op=ALU.pow)
+            centred = work.tile([P, FEAT], F32)
+            nc.vector.scalar_tensor_tensor(
+                out=centred[:], in0=z, scalar=mean_var[:, 0:1], in1=gamma_bc[:], op0=ALU.subtract, op1=ALU.mult
+            )
+            nc.vector.scalar_tensor_tensor(
+                out=y_all[:, i, :], in0=centred[:], scalar=rstd[:], in1=beta_bc[:], op0=ALU.mult, op1=ALU.add
+            )
+
+        def quantise_y(i):
+            rows = slice(i * P, (i + 1) * P)
+            for c in range(FEAT_PASSES):
+                y_grouped = work.tile([P, P, PACK], BF16, align_bytes=64, bufs=4)
+                flip_512_of_k(y_all[:, i, c * K_PASS : (c + 1) * K_PASS], ident_f32[:], F32, y_grouped[:])
+                nc.vector.quantize_mx(
+                    out=y_codes[:, c, rows].bitcast(FP8X4),
+                    scales=y_scales[:, c, rows],
+                    in_=y_grouped[:].rearrange("p r t -> p (r t)"),
+                )
+
+        def hidden_layer(n):
+            rows = slice(n * N_MAX, (n + 1) * N_MAX)
+            h_planes = work.tile([P, HID_TILES, N_MAX], BF16)
+            for m in range(HID_TILES):
+                units = slice(m * P, (m + 1) * P)
+                h_sum = sums.tile([P, N_MAX], F32, tag="sums")
+                for c in range(FEAT_PASSES):
+                    nc.tensor.matmul_mx(
+                        out=h_sum[:],
+                        lhsT=w1_codes[:, c, units].bitcast(FP8X4),
+                        lhsT_scale=w1_scales[:, c, units],
+                        rhs=y_codes[:, c, rows].bitcast(FP8X4),
+                        rhs_scale=y_scales[:, c, rows],
+                        start=(c == 0),
+                        stop=(c == FEAT_PASSES - 1),
+                    )
+                nc.scalar.activation(out=h_planes[:, m, :], in_=h_sum[:], func=ACT.Relu, bias=bias_cols[:, m : m + 1])
+            h_grouped = work.tile([P, N_MAX, PACK], BF16, align_bytes=64)
+            nc.vector.tensor_copy(out=h_grouped[:], in_=h_planes[:].rearrange("p m r -> p r m"))
+            nc.vector.quantize_mx(
+                out=h_codes[:, rows].bitcast(FP8X4),
+                scales=h_scales[:, rows],
+                in_=h_grouped[:].rearrange("p r m -> p (r m)"),
+            )
+
+        def gate_layer(n):
+            rows = slice(n * N_MAX, (n + 1) * N_MAX)
+            gate_t = work.tile([P, FEAT_TILES, N_MAX], F32)
+            for j in range(FEAT_TILES):
+                feats = slice(j * P, (j + 1) * P)
+                g_sum = sums.tile([P, N_MAX], F32, tag="sums")
+                nc.tensor.matmul_mx(
+                    out=g_sum[:],
+                    lhsT=w2_codes[:, feats].bitcast(FP8X4),
+                    lhsT_scale=w2_scales[:, feats],
+                    rhs=h_codes[:, rows].bitcast(FP8X4),
+                    rhs_scale=h_scales[:, rows],
+                    start=True,
+                    stop=True,
+                )
+                nc.scalar.activation(
+                    out=gate_t[:, j, :],
+                    in_=g_sum[:],
+                    func=ACT.Sigmoid,
+                    bias=bias_cols[:, HID_TILES + j : HID_TILES + j + 1],
+                )
+            return gate_t
+
+        def gated_output(i, gate_t):
+            r = i % TILES_PER_ROUND
+            result = work.tile([P, FEAT], F32, bufs=3)
+            for c in range(FEAT // N_MAX):
+                gate = flip.tile([P, PACK, P], F32, tag="flip")
+                for t in range(PACK):
+                    nc.tensor.transpose(gate[:, t, :], gate_t[:, c * PACK + t, r * P : (r + 1) * P], ident_f32[:])
+                feats = slice(c * N_MAX, (c + 1) * N_MAX)
+                nc.vector.tensor_tensor(
+                    out=result[:, feats],
+                    in0=gate[:].rearrange("p t f -> p (t f)"),
+                    in1=y_all[:, i, feats],
+                    op=ALU.mult,
+                )
+            nc.sync.dma_start(out=out[i * P : (i + 1) * P, :], in_=result[:])
+
+        w2_grouped = keep.tile([P, FEAT, PACK], BF16, align_bytes=64)
+        for n in range(ROUNDS):
+            tiles = range(n * TILES_PER_ROUND, (n + 1) * TILES_PER_ROUND)
+            for i in tiles:
+                layer_norm(i)
+                quantise_y(i)
+            hidden_layer(n)
+            if n == 0:
+                for j in range(FEAT_TILES):
+                    flip_512_of_k(w2_raw[:, j, :], ident_bf16[:], BF16, w2_grouped[:, j * P : (j + 1) * P, :])
+                nc.vector.quantize_mx(
+                    out=w2_codes[:].bitcast(FP8X4),
+                    scales=w2_scales[:],
+                    in_=w2_grouped[:].rearrange("p r t -> p (r t)"),
+                )
+            gate_t = gate_layer(n)
+            for i in tiles:
+                gated_output(i, gate_t)

@@ -1,3 +1,5 @@
+from contextlib import ExitStack
+
 import concourse.mybir as mybir
 from concourse.masks import make_identity
 
@@ -12,7 +14,7 @@ ACT = mybir.ActivationFunctionType
 P = 128
 PACK = 4
 K_PASS = P * PACK
-N_MAX = 512
+BANK = 512
 
 ROWS, FEAT, HID = 1024, 1024, 512
 LN_EPS = 1e-5
@@ -20,31 +22,50 @@ ROW_TILES = ROWS // P
 FEAT_TILES = FEAT // P
 HID_TILES = HID // P
 FEAT_PASSES = FEAT // K_PASS
-ROUNDS = ROWS // N_MAX
-TILES_PER_ROUND = N_MAX // P
+FEAT_BANKS = FEAT // BANK
+
+ROUND_TILES = 2
+ROUND_ROWS = ROUND_TILES * P
+ROUNDS = ROW_TILES // ROUND_TILES
+PER_BANK = BANK // ROUND_ROWS
+
+WEIGHT_QUARTERS = 4
+W2_QUARTER = FEAT_PASSES
 
 FLOPS = 2 * ROWS * FEAT * HID * 2
+
+STATS_LEAD = 2
+LAG_QUANTISE_Y = 1
+LAG_REGROUP_H = 2
+LAG_GATE = 3
+LAG_FLIP_GATE = 6
+LAG_PRODUCT = 7
 
 
 def tile_kanlayer_pb_kernel(tc, kan_sum, ln_gamma, ln_beta, se_w1, se_b1, se_w2, se_b2, out):
     nc = tc.nc
-    with tc.tile_pool(name="keep", bufs=1) as keep, tc.tile_pool(name="small", bufs=4) as small, tc.tile_pool(
-        name="work", bufs=2
-    ) as work, tc.psum_pool(name="flip", bufs=4) as flip, tc.psum_pool(name="sums", bufs=4) as sums:
+    with ExitStack() as stack:
+        keep = stack.enter_context(tc.tile_pool(name="keep", bufs=1))
+        work = stack.enter_context(tc.tile_pool(name="work", bufs=2))
+        flip = stack.enter_context(tc.psum_pool(name="flip", bufs=4))
+        sums = stack.enter_context(tc.psum_pool(name="sums", bufs=4))
+        stack.enter_context(tc.manual_schedule())
+
         z_all = keep.tile([P, ROW_TILES, FEAT], BF16)
         w1_raw = keep.tile([P, HID_TILES, FEAT], BF16)
         w2_raw = keep.tile([P, FEAT_TILES, HID], BF16)
-        for i in range(TILES_PER_ROUND):
-            nc.sync.dma_start(out=z_all[:, i, :], in_=kan_sum[i * P : (i + 1) * P, :])
+        z_tiles = kan_sum.rearrange("(i p) f -> p i f", p=P)
+        for i in range(STATS_LEAD + 1):
+            nc.sync.dma_start(out=z_all[:, i, :], in_=z_tiles[:, i, :])
         nc.sync.dma_start(out=w1_raw[:], in_=se_w1.rearrange("(m p) f -> p m f", p=P))
-        for i in range(TILES_PER_ROUND, ROW_TILES):
-            nc.sync.dma_start(out=z_all[:, i, :], in_=kan_sum[i * P : (i + 1) * P, :])
+        nc.sync.dma_start(out=z_all[:, STATS_LEAD + 1, :], in_=z_tiles[:, STATS_LEAD + 1, :])
         nc.sync.dma_start(out=w2_raw[:], in_=se_w2.rearrange("(j p) h -> p j h", p=P))
+        nc.sync.dma_start(out=z_all[:, STATS_LEAD + 2 :, :], in_=z_tiles[:, STATS_LEAD + 2 :, :])
 
-        gamma_bc = keep.tile([P, FEAT], BF16)
-        beta_bc = keep.tile([P, FEAT], BF16)
-        nc.scalar.dma_start(out=gamma_bc[:], in_=ln_gamma.partition_broadcast(P))
-        nc.scalar.dma_start(out=beta_bc[:], in_=ln_beta.partition_broadcast(P))
+        affine_rows = keep.tile([P, 2 * FEAT], BF16)
+        nc.vector.memset(affine_rows[:], 0.0)
+        nc.scalar.dma_start(out=affine_rows[0:1, 0:FEAT], in_=ln_gamma.rearrange("(o f) -> o f", o=1))
+        nc.scalar.dma_start(out=affine_rows[0:1, FEAT : 2 * FEAT], in_=ln_beta.rearrange("(o f) -> o f", o=1))
         bias_rows = keep.tile([P, P], BF16)
         nc.vector.memset(bias_rows[:], 0.0)
         nc.scalar.dma_start(out=bias_rows[0:HID_TILES, :], in_=se_b1.rearrange("(m p) -> m p", p=P))
@@ -52,27 +73,46 @@ def tile_kanlayer_pb_kernel(tc, kan_sum, ln_gamma, ln_beta, se_w1, se_b1, se_w2,
             out=bias_rows[HID_TILES : HID_TILES + FEAT_TILES, :], in_=se_b2.rearrange("(j p) -> j p", p=P)
         )
 
+        ones = keep.tile([P, P], BF16)
+        nc.gpsimd.memset(ones[:], 1.0)
+        minus_half = keep.tile([P, 1], F32)
+        nc.gpsimd.memset(minus_half[:], -0.5)
         ident_bf16 = keep.tile([P, P], BF16)
         make_identity(nc, ident_bf16[:])
         ident_f32 = keep.tile([P, P], F32)
         make_identity(nc, ident_f32[:])
-        minus_half = keep.tile([P, 1], F32)
-        nc.gpsimd.memset(minus_half[:], -0.5)
+
+        affine = keep.tile([P, 2 * FEAT], BF16)
+        for b in range(2 * FEAT_BANKS):
+            cols = slice(b * BANK, (b + 1) * BANK)
+            spread = sums.tile([P, BANK], F32, tag="sums")
+            nc.tensor.matmul(out=spread[:], lhsT=ones[:], rhs=affine_rows[:, cols], start=True, stop=True)
+            nc.scalar.copy(out=affine[:, cols], in_=spread[:])
+        gamma = affine[:, 0:FEAT]
+        beta = affine[:, FEAT : 2 * FEAT]
 
         bias_flip = flip.tile([P, P], BF16, tag="flip")
         nc.tensor.transpose(bias_flip[:], bias_rows[:], ident_bf16[:])
         bias_cols = keep.tile([P, HID_TILES + FEAT_TILES], F32)
-        nc.vector.tensor_copy(out=bias_cols[:], in_=bias_flip[:, 0 : HID_TILES + FEAT_TILES])
+        nc.scalar.copy(out=bias_cols[:], in_=bias_flip[:, 0 : HID_TILES + FEAT_TILES])
 
-        w1_codes = keep.tile([P, FEAT_PASSES, HID], U32, align_bytes=64)
-        w1_scales = keep.tile([P, FEAT_PASSES, HID], U8, align_bytes=64)
-        w2_codes = keep.tile([P, FEAT], U32, align_bytes=64)
-        w2_scales = keep.tile([P, FEAT], U8, align_bytes=64)
+        w_grouped = keep.tile([P, WEIGHT_QUARTERS, K_PASS, PACK], BF16, align_bytes=64)
+        w_codes = keep.tile([P, WEIGHT_QUARTERS, K_PASS], U32, align_bytes=64)
+        w_scales = keep.tile([P, WEIGHT_QUARTERS, K_PASS], U8, align_bytes=64)
+        y_grouped = keep.tile([P, FEAT_PASSES, ROWS, PACK], BF16, align_bytes=64)
         y_codes = keep.tile([P, FEAT_PASSES, ROWS], U32, align_bytes=64)
         y_scales = keep.tile([P, FEAT_PASSES, ROWS], U8, align_bytes=64)
+        h_planes = keep.tile([P, HID_TILES, ROWS], BF16)
+        h_grouped = keep.tile([P, ROWS, PACK], BF16, align_bytes=64)
         h_codes = keep.tile([P, ROWS], U32, align_bytes=64)
         h_scales = keep.tile([P, ROWS], U8, align_bytes=64)
+        stats = keep.tile([P, ROW_TILES, FEAT_BANKS, 6], F32)
+        mean_var = keep.tile([P, ROW_TILES, 2], F32)
+        var_eps = keep.tile([P, ROW_TILES], F32)
+        rstd = keep.tile([P, ROW_TILES], F32)
         y_all = keep.tile([P, ROW_TILES, FEAT], F32)
+        gate_t = keep.tile([P, FEAT_TILES, ROWS], F32)
+        gate_rows = {}
 
         def flip_512_of_k(src, ident, dtype, grouped):
             flipped = flip.tile([P, PACK, P], dtype, tag="flip")
@@ -80,132 +120,177 @@ def tile_kanlayer_pb_kernel(tc, kan_sum, ln_gamma, ln_beta, se_w1, se_b1, se_w2,
                 nc.tensor.transpose(flipped[:, t, :], src[:, t * P : (t + 1) * P], ident)
             nc.scalar.copy(out=grouped, in_=flipped[:].rearrange("p t r -> p r t"))
 
-        w1_grouped = keep.tile([P, FEAT_PASSES, HID, PACK], BF16, align_bytes=64)
-        for c in range(FEAT_PASSES):
-            for m in range(HID_TILES):
-                flip_512_of_k(
-                    w1_raw[:, m, c * K_PASS : (c + 1) * K_PASS],
-                    ident_bf16[:],
-                    BF16,
-                    w1_grouped[:, c, m * P : (m + 1) * P, :],
-                )
+        def flip_weights(q):
+            for b in range(PACK):
+                if q < W2_QUARTER:
+                    block = w1_raw[:, b, q * K_PASS : (q + 1) * K_PASS]
+                else:
+                    block = w2_raw[:, (q - W2_QUARTER) * PACK + b, :]
+                flip_512_of_k(block, ident_bf16[:], BF16, w_grouped[:, q, b * P : (b + 1) * P, :])
+
+        def quantise_weights(q):
             nc.vector.quantize_mx(
-                out=w1_codes[:, c, :].bitcast(FP8X4),
-                scales=w1_scales[:, c, :],
-                in_=w1_grouped[:, c, :, :].rearrange("p r t -> p (r t)"),
+                out=w_codes[:, q, :].bitcast(FP8X4),
+                scales=w_scales[:, q, :],
+                in_=w_grouped[:, q, :, :].rearrange("p r t -> p (r t)"),
             )
 
-        def layer_norm(i):
-            z = z_all[:, i, :]
-            stats = small.tile([P, FEAT // N_MAX, 6], F32)
-            for s in range(FEAT // N_MAX):
-                nc.vector.bn_stats(out=stats[:, s, :], in_=z[:, s * N_MAX : (s + 1) * N_MAX])
-            mean_var = small.tile([P, 2], F32)
-            nc.vector.bn_aggr(out=mean_var[:], in_=stats[:].rearrange("p s d -> p (s d)"))
-            var_eps = small.tile([P, 1], F32)
+        def partial_statistics(i):
+            for b in range(FEAT_BANKS):
+                nc.vector.bn_stats(out=stats[:, i, b, :], in_=z_all[:, i, b * BANK : (b + 1) * BANK])
+
+        def finish_statistics(i):
+            nc.vector.bn_aggr(out=mean_var[:, i, :], in_=stats[:, i, :, :].rearrange("p b d -> p (b d)"))
             nc.gpsimd.tensor_scalar(
-                out=var_eps[:], in0=mean_var[:, 1:2], scalar1=1.0, scalar2=LN_EPS, op0=ALU.mult, op1=ALU.add
+                out=var_eps[:, i : i + 1],
+                in0=mean_var[:, i, 1:2],
+                scalar1=1.0,
+                scalar2=LN_EPS,
+                op0=ALU.mult,
+                op1=ALU.add,
             )
-            rstd = small.tile([P, 1], F32)
-            nc.gpsimd.tensor_tensor(out=rstd[:], in0=var_eps[:], in1=minus_half[:], op=ALU.pow)
+            nc.gpsimd.tensor_tensor(out=rstd[:, i : i + 1], in0=var_eps[:, i : i + 1], in1=minus_half[:], op=ALU.pow)
+
+        def centre(i):
             centred = work.tile([P, FEAT], F32)
             nc.vector.scalar_tensor_tensor(
-                out=centred[:], in0=z, scalar=mean_var[:, 0:1], in1=gamma_bc[:], op0=ALU.subtract, op1=ALU.mult
+                out=centred[:],
+                in0=z_all[:, i, :],
+                scalar=mean_var[:, i, 0:1],
+                in1=gamma,
+                op0=ALU.subtract,
+                op1=ALU.mult,
             )
+            return centred
+
+        def scale_and_flip(i, centred):
             nc.vector.scalar_tensor_tensor(
-                out=y_all[:, i, :], in0=centred[:], scalar=rstd[:], in1=beta_bc[:], op0=ALU.mult, op1=ALU.add
+                out=y_all[:, i, :], in0=centred[:], scalar=rstd[:, i : i + 1], in1=beta, op0=ALU.mult, op1=ALU.add
             )
+            for c in range(FEAT_PASSES):
+                flip_512_of_k(
+                    y_all[:, i, c * K_PASS : (c + 1) * K_PASS],
+                    ident_f32[:],
+                    F32,
+                    y_grouped[:, c, i * P : (i + 1) * P, :],
+                )
 
         def quantise_y(i):
             rows = slice(i * P, (i + 1) * P)
             for c in range(FEAT_PASSES):
-                y_grouped = work.tile([P, P, PACK], BF16, align_bytes=64, bufs=4)
-                flip_512_of_k(y_all[:, i, c * K_PASS : (c + 1) * K_PASS], ident_f32[:], F32, y_grouped[:])
                 nc.vector.quantize_mx(
                     out=y_codes[:, c, rows].bitcast(FP8X4),
                     scales=y_scales[:, c, rows],
-                    in_=y_grouped[:].rearrange("p r t -> p (r t)"),
+                    in_=y_grouped[:, c, rows, :].rearrange("p r t -> p (r t)"),
                 )
 
         def hidden_layer(n):
-            rows = slice(n * N_MAX, (n + 1) * N_MAX)
-            h_planes = work.tile([P, HID_TILES, N_MAX], BF16)
-            for m in range(HID_TILES):
-                units = slice(m * P, (m + 1) * P)
-                h_sum = sums.tile([P, N_MAX], F32, tag="sums")
-                for c in range(FEAT_PASSES):
-                    nc.tensor.matmul_mx(
-                        out=h_sum[:],
-                        lhsT=w1_codes[:, c, units].bitcast(FP8X4),
-                        lhsT_scale=w1_scales[:, c, units],
-                        rhs=y_codes[:, c, rows].bitcast(FP8X4),
-                        rhs_scale=y_scales[:, c, rows],
-                        start=(c == 0),
-                        stop=(c == FEAT_PASSES - 1),
+            rows = slice(n * ROUND_ROWS, (n + 1) * ROUND_ROWS)
+            for first in range(0, HID_TILES, PER_BANK):
+                h_sum = sums.tile([P, PER_BANK, ROUND_ROWS], F32, tag="sums")
+                for g in range(PER_BANK):
+                    units = slice((first + g) * P, (first + g + 1) * P)
+                    for c in range(FEAT_PASSES):
+                        nc.tensor.matmul_mx(
+                            out=h_sum[:, g, :],
+                            lhsT=w_codes[:, c, units].bitcast(FP8X4),
+                            lhsT_scale=w_scales[:, c, units],
+                            rhs=y_codes[:, c, rows].bitcast(FP8X4),
+                            rhs_scale=y_scales[:, c, rows],
+                            start=(c == 0),
+                            stop=(c == FEAT_PASSES - 1),
+                        )
+                for g in range(PER_BANK):
+                    m = first + g
+                    nc.scalar.activation(
+                        out=h_planes[:, m, rows], in_=h_sum[:, g, :], func=ACT.Relu, bias=bias_cols[:, m : m + 1]
                     )
-                nc.scalar.activation(out=h_planes[:, m, :], in_=h_sum[:], func=ACT.Relu, bias=bias_cols[:, m : m + 1])
-            h_grouped = work.tile([P, N_MAX, PACK], BF16, align_bytes=64)
-            nc.vector.tensor_copy(out=h_grouped[:], in_=h_planes[:].rearrange("p m r -> p r m"))
+
+        def regroup_h(n):
+            rows = slice(n * ROUND_ROWS, (n + 1) * ROUND_ROWS)
+            nc.vector.tensor_copy(out=h_grouped[:, rows, :], in_=h_planes[:, :, rows].rearrange("p m r -> p r m"))
+
+        def gate_layer(n):
+            rows = slice(n * ROUND_ROWS, (n + 1) * ROUND_ROWS)
             nc.vector.quantize_mx(
                 out=h_codes[:, rows].bitcast(FP8X4),
                 scales=h_scales[:, rows],
-                in_=h_grouped[:].rearrange("p r m -> p (r m)"),
+                in_=h_grouped[:, rows, :].rearrange("p r m -> p (r m)"),
             )
+            for first in range(0, FEAT_TILES, PER_BANK):
+                g_sum = sums.tile([P, PER_BANK, ROUND_ROWS], F32, tag="sums")
+                for g in range(PER_BANK):
+                    j = first + g
+                    q = W2_QUARTER + j // PACK
+                    feats = slice((j % PACK) * P, (j % PACK + 1) * P)
+                    nc.tensor.matmul_mx(
+                        out=g_sum[:, g, :],
+                        lhsT=w_codes[:, q, feats].bitcast(FP8X4),
+                        lhsT_scale=w_scales[:, q, feats],
+                        rhs=h_codes[:, rows].bitcast(FP8X4),
+                        rhs_scale=h_scales[:, rows],
+                        start=True,
+                        stop=True,
+                    )
+                for g in range(PER_BANK):
+                    j = first + g
+                    nc.scalar.activation(
+                        out=gate_t[:, j, rows],
+                        in_=g_sum[:, g, :],
+                        func=ACT.Sigmoid,
+                        bias=bias_cols[:, HID_TILES + j : HID_TILES + j + 1],
+                    )
 
-        def gate_layer(n):
-            rows = slice(n * N_MAX, (n + 1) * N_MAX)
-            gate_t = work.tile([P, FEAT_TILES, N_MAX], F32)
-            for j in range(FEAT_TILES):
-                feats = slice(j * P, (j + 1) * P)
-                g_sum = sums.tile([P, N_MAX], F32, tag="sums")
-                nc.tensor.matmul_mx(
-                    out=g_sum[:],
-                    lhsT=w2_codes[:, feats].bitcast(FP8X4),
-                    lhsT_scale=w2_scales[:, feats],
-                    rhs=h_codes[:, rows].bitcast(FP8X4),
-                    rhs_scale=h_scales[:, rows],
-                    start=True,
-                    stop=True,
-                )
-                nc.scalar.activation(
-                    out=gate_t[:, j, :],
-                    in_=g_sum[:],
-                    func=ACT.Sigmoid,
-                    bias=bias_cols[:, HID_TILES + j : HID_TILES + j + 1],
-                )
-            return gate_t
-
-        def gated_output(i, gate_t):
-            r = i % TILES_PER_ROUND
-            result = work.tile([P, FEAT], F32, bufs=3)
-            for c in range(FEAT // N_MAX):
-                gate = flip.tile([P, PACK, P], F32, tag="flip")
+        def flip_gate(i):
+            for b in range(FEAT_BANKS):
+                flipped = flip.tile([P, PACK, P], F32, tag="flip", name="gate_rows_%d_%d" % (i, b))
                 for t in range(PACK):
-                    nc.tensor.transpose(gate[:, t, :], gate_t[:, c * PACK + t, r * P : (r + 1) * P], ident_f32[:])
-                feats = slice(c * N_MAX, (c + 1) * N_MAX)
+                    nc.tensor.transpose(flipped[:, t, :], gate_t[:, b * PACK + t, i * P : (i + 1) * P], ident_f32[:])
+                gate_rows[(i, b)] = flipped
+
+        def gated_output(i):
+            for b in range(FEAT_BANKS):
+                feats = slice(b * BANK, (b + 1) * BANK)
+                result = work.tile([P, BANK], F32, bufs=4)
                 nc.vector.tensor_tensor(
-                    out=result[:, feats],
-                    in0=gate[:].rearrange("p t f -> p (t f)"),
+                    out=result[:],
+                    in0=gate_rows[(i, b)][:].rearrange("p t f -> p (t f)"),
                     in1=y_all[:, i, feats],
                     op=ALU.mult,
                 )
-            nc.sync.dma_start(out=out[i * P : (i + 1) * P, :], in_=result[:])
+                nc.sync.dma_start(out=out[i * P : (i + 1) * P, feats], in_=result[:])
 
-        w2_grouped = keep.tile([P, FEAT, PACK], BF16, align_bytes=64)
-        for n in range(ROUNDS):
-            tiles = range(n * TILES_PER_ROUND, (n + 1) * TILES_PER_ROUND)
-            for i in tiles:
-                layer_norm(i)
-                quantise_y(i)
-            hidden_layer(n)
-            if n == 0:
-                for j in range(FEAT_TILES):
-                    flip_512_of_k(w2_raw[:, j, :], ident_bf16[:], BF16, w2_grouped[:, j * P : (j + 1) * P, :])
-                nc.vector.quantize_mx(
-                    out=w2_codes[:].bitcast(FP8X4),
-                    scales=w2_scales[:],
-                    in_=w2_grouped[:].rearrange("p r t -> p (r t)"),
-                )
-            gate_t = gate_layer(n)
-            for i in tiles:
-                gated_output(i, gate_t)
+        def round_that_ends_with(i):
+            if 0 <= i < ROW_TILES and i % ROUND_TILES == ROUND_TILES - 1:
+                return i // ROUND_TILES
+            return None
+
+        for i in range(STATS_LEAD):
+            partial_statistics(i)
+            finish_statistics(i)
+        flip_weights(0)
+        for s in range(ROW_TILES + LAG_PRODUCT):
+            if s + 1 < WEIGHT_QUARTERS:
+                flip_weights(s + 1)
+            if 0 <= s - LAG_PRODUCT:
+                gated_output(s - LAG_PRODUCT)
+            if 0 <= s - LAG_FLIP_GATE < ROW_TILES:
+                flip_gate(s - LAG_FLIP_GATE)
+            if s < ROW_TILES:
+                centred = centre(s)
+            if s + STATS_LEAD < ROW_TILES:
+                partial_statistics(s + STATS_LEAD)
+            if 0 <= s - 1 < WEIGHT_QUARTERS:
+                quantise_weights(s - 1)
+            if 0 <= s - LAG_QUANTISE_Y < ROW_TILES:
+                quantise_y(s - LAG_QUANTISE_Y)
+            if round_that_ends_with(s - LAG_QUANTISE_Y) is not None:
+                hidden_layer(round_that_ends_with(s - LAG_QUANTISE_Y))
+            if s < ROW_TILES:
+                scale_and_flip(s, centred)
+            if s + STATS_LEAD < ROW_TILES:
+                finish_statistics(s + STATS_LEAD)
+            if round_that_ends_with(s - LAG_REGROUP_H) is not None:
+                regroup_h(round_that_ends_with(s - LAG_REGROUP_H))
+            if round_that_ends_with(s - LAG_GATE) is not None:
+                gate_layer(round_that_ends_with(s - LAG_GATE))

@@ -13,14 +13,15 @@ ACT = mybir.ActivationFunctionType
 
 P = 128
 PACK = 4
+PAIR = 2
 K_PASS = P * PACK
 BANK = 512
 
 ROWS, FEAT, HID = 1024, 1024, 512
 LN_EPS = 1e-5
 ROW_TILES = ROWS // P
-FEAT_TILES = FEAT // P
-HID_TILES = HID // P
+FEAT_BLOCKS = FEAT // P
+HID_BLOCKS = HID // P
 FEAT_PASSES = FEAT // K_PASS
 FEAT_BANKS = FEAT // BANK
 
@@ -29,268 +30,275 @@ ROUND_ROWS = ROUND_TILES * P
 ROUNDS = ROW_TILES // ROUND_TILES
 PER_BANK = BANK // ROUND_ROWS
 
-WEIGHT_QUARTERS = 4
-W2_QUARTER = FEAT_PASSES
+LAYERS = 2
+LAYER_WORDS = FEAT * HID // K_PASS
+
+GAMMA, BETA, B2, B1 = 0, FEAT_BLOCKS, 2 * FEAT_BLOCKS, 3 * FEAT_BLOCKS
+VEC_COLS = 3 * FEAT_BLOCKS + HID_BLOCKS
 
 FLOPS = 2 * ROWS * FEAT * HID * 2
 
-STATS_LEAD = 2
-LAG_QUANTISE_Y = 1
-LAG_REGROUP_H = 2
-LAG_GATE = 3
-LAG_FLIP_GATE = 6
-LAG_PRODUCT = 7
+STATS_GROUP = 2
+LAG_HIDDEN = 2
+LAG_GATE = 4
+RESULT_TILES = 6
 
 
 def tile_kanlayer_pb_kernel(tc, kan_sum, ln_gamma, ln_beta, se_w1, se_b1, se_w2, se_b2, out):
     nc = tc.nc
     with ExitStack() as stack:
         keep = stack.enter_context(tc.tile_pool(name="keep", bufs=1))
-        work = stack.enter_context(tc.tile_pool(name="work", bufs=2))
+        work = stack.enter_context(tc.tile_pool(name="work", bufs=2 * ROUND_TILES))
         flip = stack.enter_context(tc.psum_pool(name="flip", bufs=4))
         sums = stack.enter_context(tc.psum_pool(name="sums", bufs=4))
         stack.enter_context(tc.manual_schedule())
 
         z_all = keep.tile([P, ROW_TILES, FEAT], BF16)
-        w1_raw = keep.tile([P, HID_TILES, FEAT], BF16)
-        w2_raw = keep.tile([P, FEAT_TILES, HID], BF16)
+        w1_raw = keep.tile([P, HID_BLOCKS, FEAT], BF16)
+        w2_raw = keep.tile([P, FEAT_BLOCKS, HID], BF16)
         z_tiles = kan_sum.rearrange("(i p) f -> p i f", p=P)
-        for i in range(STATS_LEAD + 1):
+        for i in range(ROUND_TILES):
             nc.sync.dma_start(out=z_all[:, i, :], in_=z_tiles[:, i, :])
-        nc.sync.dma_start(out=w1_raw[:], in_=se_w1.rearrange("(m p) f -> p m f", p=P))
-        nc.sync.dma_start(out=z_all[:, STATS_LEAD + 1, :], in_=z_tiles[:, STATS_LEAD + 1, :])
-        nc.sync.dma_start(out=w2_raw[:], in_=se_w2.rearrange("(j p) h -> p j h", p=P))
-        nc.sync.dma_start(out=z_all[:, STATS_LEAD + 2 :, :], in_=z_tiles[:, STATS_LEAD + 2 :, :])
-
-        affine_rows = keep.tile([P, 2 * FEAT], BF16)
-        nc.vector.memset(affine_rows[:], 0.0)
-        nc.scalar.dma_start(out=affine_rows[0:1, 0:FEAT], in_=ln_gamma.rearrange("(o f) -> o f", o=1))
-        nc.scalar.dma_start(out=affine_rows[0:1, FEAT : 2 * FEAT], in_=ln_beta.rearrange("(o f) -> o f", o=1))
-        bias_rows = keep.tile([P, P], BF16)
-        nc.vector.memset(bias_rows[:], 0.0)
-        nc.scalar.dma_start(out=bias_rows[0:HID_TILES, :], in_=se_b1.rearrange("(m p) -> m p", p=P))
-        nc.scalar.dma_start(
-            out=bias_rows[HID_TILES : HID_TILES + FEAT_TILES, :], in_=se_b2.rearrange("(j p) -> j p", p=P)
+        nc.sync.dma_start(
+            out=w1_raw[:].rearrange("q (a e) f -> q a e f", e=PAIR),
+            in_=se_w1.rearrange("(a q e) f -> q a e f", q=P, e=PAIR),
         )
+        for i in range(ROUND_TILES, STATS_GROUP * ROUND_TILES):
+            nc.sync.dma_start(out=z_all[:, i, :], in_=z_tiles[:, i, :])
+        nc.sync.dma_start(
+            out=w2_raw[:].rearrange("q (a e) h -> q a e h", e=PAIR),
+            in_=se_w2.rearrange("(a q e) h -> q a e h", q=P, e=PAIR),
+        )
+        nc.sync.dma_start(out=z_all[:, STATS_GROUP * ROUND_TILES :, :], in_=z_tiles[:, STATS_GROUP * ROUND_TILES :, :])
 
-        ones = keep.tile([P, P], BF16)
-        nc.gpsimd.memset(ones[:], 1.0)
+        vec_rows = keep.tile([P, PAIR * P], BF16)
+        nc.vector.memset(vec_rows[:], 0.0)
+        for first_col, vec in ((GAMMA, ln_gamma), (BETA, ln_beta), (B2, se_b2), (B1, se_b1)):
+            rows_of_vec = vec.rearrange("(a w) -> a w", w=PAIR * P)
+            first_row = first_col // PAIR
+            nc.scalar.dma_start(out=vec_rows[first_row : first_row + rows_of_vec.shape[0], :], in_=rows_of_vec)
+
         minus_half = keep.tile([P, 1], F32)
         nc.gpsimd.memset(minus_half[:], -0.5)
-        ident_bf16 = keep.tile([P, P], BF16)
-        make_identity(nc, ident_bf16[:])
-        ident_f32 = keep.tile([P, P], F32)
-        make_identity(nc, ident_f32[:])
+        ident = keep.tile([P, P], F32)
+        make_identity(nc, ident[:])
+        table_warmer = keep.tile([P, 1], F32)
+        nc.scalar.activation(out=table_warmer[:], in_=minus_half[:], func=ACT.Sigmoid)
 
-        affine = keep.tile([P, 2 * FEAT], BF16)
-        for b in range(2 * FEAT_BANKS):
-            cols = slice(b * BANK, (b + 1) * BANK)
-            spread = sums.tile([P, BANK], F32, tag="sums")
-            nc.tensor.matmul(out=spread[:], lhsT=ones[:], rhs=affine_rows[:, cols], start=True, stop=True)
-            nc.scalar.copy(out=affine[:, cols], in_=spread[:])
-        gamma = affine[:, 0:FEAT]
-        beta = affine[:, FEAT : 2 * FEAT]
+        vec_flip = flip.tile([P, P], F32, tag="flip")
+        nc.tensor.transpose(vec_flip[:], vec_rows[:].bitcast(F32), ident[:])
+        vec_cols = keep.tile([P, VEC_COLS], F32)
+        nc.scalar.copy(out=vec_cols[:], in_=vec_flip[:].bitcast(BF16)[:, 0:VEC_COLS])
 
-        bias_flip = flip.tile([P, P], BF16, tag="flip")
-        nc.tensor.transpose(bias_flip[:], bias_rows[:], ident_bf16[:])
-        bias_cols = keep.tile([P, HID_TILES + FEAT_TILES], F32)
-        nc.scalar.copy(out=bias_cols[:], in_=bias_flip[:, 0 : HID_TILES + FEAT_TILES])
-
-        w_grouped = keep.tile([P, WEIGHT_QUARTERS, K_PASS, PACK], BF16, align_bytes=64)
-        w_codes = keep.tile([P, WEIGHT_QUARTERS, K_PASS], U32, align_bytes=64)
-        w_scales = keep.tile([P, WEIGHT_QUARTERS, K_PASS], U8, align_bytes=64)
-        y_grouped = keep.tile([P, FEAT_PASSES, ROWS, PACK], BF16, align_bytes=64)
-        y_codes = keep.tile([P, FEAT_PASSES, ROWS], U32, align_bytes=64)
-        y_scales = keep.tile([P, FEAT_PASSES, ROWS], U8, align_bytes=64)
-        h_planes = keep.tile([P, HID_TILES, ROWS], BF16)
+        w_grouped = keep.tile([P, LAYERS * LAYER_WORDS * PACK], BF16, align_bytes=64)
+        w_codes = keep.tile([P, LAYERS * LAYER_WORDS], U32, align_bytes=64)
+        w_scales = keep.tile([P, LAYERS * LAYER_WORDS], U8, align_bytes=64)
+        y_t = keep.tile([P, FEAT_BLOCKS, ROWS], F32)
+        y_grouped = keep.tile([P, ROUNDS, FEAT_PASSES, ROUND_ROWS, PACK], BF16, align_bytes=64)
+        y_codes = keep.tile([P, ROUNDS, FEAT_PASSES, ROUND_ROWS], U32, align_bytes=64)
+        y_scales = keep.tile([P, ROUNDS, FEAT_PASSES, ROUND_ROWS], U8, align_bytes=64)
+        h_planes = keep.tile([P, HID_BLOCKS, ROWS], BF16)
         h_grouped = keep.tile([P, ROWS, PACK], BF16, align_bytes=64)
         h_codes = keep.tile([P, ROWS], U32, align_bytes=64)
         h_scales = keep.tile([P, ROWS], U8, align_bytes=64)
+        gate_t = keep.tile([P, FEAT_BLOCKS, ROWS], F32)
         stats = keep.tile([P, ROW_TILES, FEAT_BANKS, 6], F32)
         mean_var = keep.tile([P, ROW_TILES, 2], F32)
         var_eps = keep.tile([P, ROW_TILES], F32)
         rstd = keep.tile([P, ROW_TILES], F32)
-        y_all = keep.tile([P, ROW_TILES, FEAT], F32)
-        gate_t = keep.tile([P, FEAT_TILES, ROWS], F32)
-        gate_rows = {}
 
-        def flip_512_of_k(src, ident, dtype, grouped):
-            flipped = flip.tile([P, PACK, P], dtype, tag="flip")
-            for t in range(PACK):
-                nc.tensor.transpose(flipped[:, t, :], src[:, t * P : (t + 1) * P], ident)
-            nc.scalar.copy(out=grouped, in_=flipped[:].rearrange("p t r -> p r t"))
+        w_grouped_words = w_grouped[:].bitcast(F32).rearrange("p (r u) -> p r u", u=PAIR)
+        w1_words = w1_raw[:].rearrange("q m f -> q (m f)").bitcast(F32).rearrange("q (m w) -> q m w", m=HID_BLOCKS)
+        w2_words = w2_raw[:].rearrange("q j h -> q (j h)").bitcast(F32).rearrange("q (j w) -> q j w", j=FEAT_BLOCKS)
+        PASS_WORDS = K_PASS // PAIR
 
-        def flip_weights(q):
-            for b in range(PACK):
-                if q < W2_QUARTER:
-                    block = w1_raw[:, b, q * K_PASS : (q + 1) * K_PASS]
-                else:
-                    block = w2_raw[:, (q - W2_QUARTER) * PACK + b, :]
-                flip_512_of_k(block, ident_bf16[:], BF16, w_grouped[:, q, b * P : (b + 1) * P, :])
+        def stationary_blocks(layer):
+            if layer == 0:
+                return [
+                    w1_words[:, m, c * PASS_WORDS : (c + 1) * PASS_WORDS]
+                    for c in range(FEAT_PASSES)
+                    for m in range(HID_BLOCKS)
+                ]
+            return [w2_words[:, j, :] for j in range(FEAT_BLOCKS)]
 
-        def quantise_weights(q):
+        def flip_layer(layer):
+            blocks = stationary_blocks(layer)
+            for first in range(0, len(blocks), PAIR):
+                flipped = flip.tile([P, PAIR, PAIR, P], F32, tag="flip")
+                for b in range(PAIR):
+                    for u in range(PAIR):
+                        nc.tensor.transpose(flipped[:, b, u, :], blocks[first + b][:, u * P : (u + 1) * P], ident[:])
+                words = slice(layer * LAYER_WORDS + first * P, layer * LAYER_WORDS + (first + PAIR) * P)
+                nc.scalar.copy(
+                    out=w_grouped_words[:, words, :].rearrange("p (b r) u -> p b r u", b=PAIR),
+                    in_=flipped[:].rearrange("p b u r -> p b r u"),
+                )
+
+        def quantise_layer(layer):
+            words = slice(layer * LAYER_WORDS, (layer + 1) * LAYER_WORDS)
             nc.vector.quantize_mx(
-                out=w_codes[:, q, :].bitcast(FP8X4),
-                scales=w_scales[:, q, :],
-                in_=w_grouped[:, q, :, :].rearrange("p r t -> p (r t)"),
+                out=w_codes[:, words].bitcast(FP8X4),
+                scales=w_scales[:, words],
+                in_=w_grouped[:, layer * LAYER_WORDS * PACK : (layer + 1) * LAYER_WORDS * PACK],
             )
 
-        def partial_statistics(i):
-            for b in range(FEAT_BANKS):
-                nc.vector.bn_stats(out=stats[:, i, b, :], in_=z_all[:, i, b * BANK : (b + 1) * BANK])
+        def tiles_of(n):
+            return range(n * ROUND_TILES, (n + 1) * ROUND_TILES)
 
-        def finish_statistics(i):
-            nc.vector.bn_aggr(out=mean_var[:, i, :], in_=stats[:, i, :, :].rearrange("p b d -> p (b d)"))
-            nc.gpsimd.tensor_scalar(
-                out=var_eps[:, i : i + 1],
-                in0=mean_var[:, i, 1:2],
-                scalar1=1.0,
-                scalar2=LN_EPS,
-                op0=ALU.mult,
-                op1=ALU.add,
-            )
-            nc.gpsimd.tensor_tensor(out=rstd[:, i : i + 1], in0=var_eps[:, i : i + 1], in1=minus_half[:], op=ALU.pow)
+        def rows_of(n):
+            return slice(n * ROUND_ROWS, (n + 1) * ROUND_ROWS)
 
-        def centre(i):
-            centred = work.tile([P, FEAT], F32)
-            nc.vector.scalar_tensor_tensor(
-                out=centred[:],
-                in0=z_all[:, i, :],
-                scalar=mean_var[:, i, 0:1],
-                in1=gamma,
+        def statistics(n):
+            for i in tiles_of(n):
+                for b in range(FEAT_BANKS):
+                    nc.vector.bn_stats(out=stats[:, i, b, :], in_=z_all[:, i, b * BANK : (b + 1) * BANK])
+            for i in tiles_of(n):
+                nc.vector.bn_aggr(out=mean_var[:, i, :], in_=stats[:, i, :, :].rearrange("p b d -> p (b d)"))
+                nc.gpsimd.tensor_scalar(
+                    out=var_eps[:, i : i + 1],
+                    in0=mean_var[:, i, 1:2],
+                    scalar1=1.0,
+                    scalar2=LN_EPS,
+                    op0=ALU.mult,
+                    op1=ALU.add,
+                )
+                nc.gpsimd.tensor_tensor(out=rstd[:, i : i + 1], in0=var_eps[:, i : i + 1], in1=minus_half[:], op=ALU.pow)
+
+        def normalise(i):
+            xhat = work.tile([P, FEAT_BLOCKS, P], F32)
+            nc.vector.tensor_scalar(
+                out=xhat[:].rearrange("p (a e) q -> p a e q", e=PAIR),
+                in0=z_all[:, i, :].rearrange("p (a q e) -> p a e q", q=P, e=PAIR),
+                scalar1=mean_var[:, i, 0:1],
+                scalar2=rstd[:, i : i + 1],
                 op0=ALU.subtract,
                 op1=ALU.mult,
             )
-            return centred
+            return xhat
 
-        def scale_and_flip(i, centred):
-            nc.vector.scalar_tensor_tensor(
-                out=y_all[:, i, :], in0=centred[:], scalar=rstd[:, i : i + 1], in1=beta, op0=ALU.mult, op1=ALU.add
+        def layer_norm(n):
+            xhats = [normalise(i) for i in tiles_of(n)]
+            for first in range(0, FEAT_BLOCKS, PER_BANK):
+                flipped = flip.tile([P, PER_BANK, ROUND_ROWS], F32, tag="flip")
+                for g in range(PER_BANK):
+                    for a in range(ROUND_TILES):
+                        nc.tensor.transpose(flipped[:, g, a * P : (a + 1) * P], xhats[a][:, first + g, :], ident[:])
+                for g in range(PER_BANK):
+                    j = first + g
+                    nc.scalar.activation(
+                        out=y_t[:, j, rows_of(n)],
+                        in_=flipped[:, g, :],
+                        func=ACT.Identity,
+                        scale=vec_cols[:, GAMMA + j : GAMMA + j + 1],
+                        bias=vec_cols[:, BETA + j : BETA + j + 1],
+                    )
+
+        def regroup_y(n):
+            nc.vector.tensor_copy(
+                out=y_grouped[:, n], in_=y_t[:, :, rows_of(n)].rearrange("p (c t) r -> p c r t", t=PACK)
             )
-            for c in range(FEAT_PASSES):
-                flip_512_of_k(
-                    y_all[:, i, c * K_PASS : (c + 1) * K_PASS],
-                    ident_f32[:],
-                    F32,
-                    y_grouped[:, c, i * P : (i + 1) * P, :],
-                )
 
-        def quantise_y(i):
-            rows = slice(i * P, (i + 1) * P)
-            for c in range(FEAT_PASSES):
-                nc.vector.quantize_mx(
-                    out=y_codes[:, c, rows].bitcast(FP8X4),
-                    scales=y_scales[:, c, rows],
-                    in_=y_grouped[:, c, rows, :].rearrange("p r t -> p (r t)"),
-                )
+        def quantise_y(n):
+            nc.vector.quantize_mx(
+                out=y_codes[:, n].rearrange("p c r -> p (c r)").bitcast(FP8X4),
+                scales=y_scales[:, n].rearrange("p c r -> p (c r)"),
+                in_=y_grouped[:, n].rearrange("p c r t -> p (c r t)"),
+            )
 
         def hidden_layer(n):
-            rows = slice(n * ROUND_ROWS, (n + 1) * ROUND_ROWS)
-            for first in range(0, HID_TILES, PER_BANK):
+            for first in range(0, HID_BLOCKS, PER_BANK):
                 h_sum = sums.tile([P, PER_BANK, ROUND_ROWS], F32, tag="sums")
                 for g in range(PER_BANK):
-                    units = slice((first + g) * P, (first + g + 1) * P)
                     for c in range(FEAT_PASSES):
+                        units = slice((c * HID_BLOCKS + first + g) * P, (c * HID_BLOCKS + first + g + 1) * P)
                         nc.tensor.matmul_mx(
                             out=h_sum[:, g, :],
-                            lhsT=w_codes[:, c, units].bitcast(FP8X4),
-                            lhsT_scale=w_scales[:, c, units],
-                            rhs=y_codes[:, c, rows].bitcast(FP8X4),
-                            rhs_scale=y_scales[:, c, rows],
+                            lhsT=w_codes[:, units].bitcast(FP8X4),
+                            lhsT_scale=w_scales[:, units],
+                            rhs=y_codes[:, n, c, :].bitcast(FP8X4),
+                            rhs_scale=y_scales[:, n, c, :],
                             start=(c == 0),
                             stop=(c == FEAT_PASSES - 1),
                         )
                 for g in range(PER_BANK):
                     m = first + g
                     nc.scalar.activation(
-                        out=h_planes[:, m, rows], in_=h_sum[:, g, :], func=ACT.Relu, bias=bias_cols[:, m : m + 1]
+                        out=h_planes[:, m, rows_of(n)],
+                        in_=h_sum[:, g, :],
+                        func=ACT.Relu,
+                        bias=vec_cols[:, B1 + m : B1 + m + 1],
                     )
 
         def regroup_h(n):
-            rows = slice(n * ROUND_ROWS, (n + 1) * ROUND_ROWS)
-            nc.vector.tensor_copy(out=h_grouped[:, rows, :], in_=h_planes[:, :, rows].rearrange("p m r -> p r m"))
+            nc.vector.tensor_copy(
+                out=h_grouped[:, rows_of(n), :], in_=h_planes[:, :, rows_of(n)].rearrange("p m r -> p r m")
+            )
+
+        def quantise_h(n):
+            nc.vector.quantize_mx(
+                out=h_codes[:, rows_of(n)].bitcast(FP8X4),
+                scales=h_scales[:, rows_of(n)],
+                in_=h_grouped[:, rows_of(n), :].rearrange("p r m -> p (r m)"),
+            )
 
         def gate_layer(n):
-            rows = slice(n * ROUND_ROWS, (n + 1) * ROUND_ROWS)
-            nc.vector.quantize_mx(
-                out=h_codes[:, rows].bitcast(FP8X4),
-                scales=h_scales[:, rows],
-                in_=h_grouped[:, rows, :].rearrange("p r m -> p (r m)"),
-            )
-            for first in range(0, FEAT_TILES, PER_BANK):
+            for first in range(0, FEAT_BLOCKS, PER_BANK):
                 g_sum = sums.tile([P, PER_BANK, ROUND_ROWS], F32, tag="sums")
                 for g in range(PER_BANK):
-                    j = first + g
-                    q = W2_QUARTER + j // PACK
-                    feats = slice((j % PACK) * P, (j % PACK + 1) * P)
+                    feats = slice(LAYER_WORDS + (first + g) * P, LAYER_WORDS + (first + g + 1) * P)
                     nc.tensor.matmul_mx(
                         out=g_sum[:, g, :],
-                        lhsT=w_codes[:, q, feats].bitcast(FP8X4),
-                        lhsT_scale=w_scales[:, q, feats],
-                        rhs=h_codes[:, rows].bitcast(FP8X4),
-                        rhs_scale=h_scales[:, rows],
+                        lhsT=w_codes[:, feats].bitcast(FP8X4),
+                        lhsT_scale=w_scales[:, feats],
+                        rhs=h_codes[:, rows_of(n)].bitcast(FP8X4),
+                        rhs_scale=h_scales[:, rows_of(n)],
                         start=True,
                         stop=True,
                     )
                 for g in range(PER_BANK):
                     j = first + g
                     nc.scalar.activation(
-                        out=gate_t[:, j, rows],
+                        out=gate_t[:, j, rows_of(n)],
                         in_=g_sum[:, g, :],
                         func=ACT.Sigmoid,
-                        bias=bias_cols[:, HID_TILES + j : HID_TILES + j + 1],
+                        bias=vec_cols[:, B2 + j : B2 + j + 1],
                     )
 
-        def flip_gate(i):
-            for b in range(FEAT_BANKS):
-                flipped = flip.tile([P, PACK, P], F32, tag="flip", name="gate_rows_%d_%d" % (i, b))
-                for t in range(PACK):
-                    nc.tensor.transpose(flipped[:, t, :], gate_t[:, b * PACK + t, i * P : (i + 1) * P], ident_f32[:])
-                gate_rows[(i, b)] = flipped
+        def gated_output(n):
+            for i in tiles_of(n):
+                rows = slice(i * P, (i + 1) * P)
+                nc.vector.tensor_tensor(out=gate_t[:, :, rows], in0=gate_t[:, :, rows], in1=y_t[:, :, rows], op=ALU.mult)
+                result = work.tile([P, FEAT], F32, bufs=RESULT_TILES)
+                for b in range(FEAT_BANKS):
+                    back = flip.tile([P, PACK, P], F32, tag="flip")
+                    for g in range(PACK):
+                        nc.tensor.transpose(back[:, g, :], gate_t[:, b * PACK + g, rows], ident[:])
+                    nc.scalar.copy(
+                        out=result[:, b * BANK : (b + 1) * BANK].rearrange("p (a q e) -> p a q e", q=P, e=PAIR),
+                        in_=back[:].rearrange("p (a e) q -> p a q e", e=PAIR),
+                    )
+                nc.sync.dma_start(out=out[rows, :], in_=result[:])
 
-        def gated_output(i):
-            for b in range(FEAT_BANKS):
-                feats = slice(b * BANK, (b + 1) * BANK)
-                result = work.tile([P, BANK], F32, bufs=4)
-                nc.vector.tensor_tensor(
-                    out=result[:],
-                    in0=gate_rows[(i, b)][:].rearrange("p t f -> p (t f)"),
-                    in1=y_all[:, i, feats],
-                    op=ALU.mult,
-                )
-                nc.sync.dma_start(out=out[i * P : (i + 1) * P, feats], in_=result[:])
-
-        def round_that_ends_with(i):
-            if 0 <= i < ROW_TILES and i % ROUND_TILES == ROUND_TILES - 1:
-                return i // ROUND_TILES
-            return None
-
-        for i in range(STATS_LEAD):
-            partial_statistics(i)
-            finish_statistics(i)
-        flip_weights(0)
-        for s in range(ROW_TILES + LAG_PRODUCT):
-            if s + 1 < WEIGHT_QUARTERS:
-                flip_weights(s + 1)
-            if 0 <= s - LAG_PRODUCT:
-                gated_output(s - LAG_PRODUCT)
-            if 0 <= s - LAG_FLIP_GATE < ROW_TILES:
-                flip_gate(s - LAG_FLIP_GATE)
-            if s < ROW_TILES:
-                centred = centre(s)
-            if s + STATS_LEAD < ROW_TILES:
-                partial_statistics(s + STATS_LEAD)
-            if 0 <= s - 1 < WEIGHT_QUARTERS:
-                quantise_weights(s - 1)
-            if 0 <= s - LAG_QUANTISE_Y < ROW_TILES:
-                quantise_y(s - LAG_QUANTISE_Y)
-            if round_that_ends_with(s - LAG_QUANTISE_Y) is not None:
-                hidden_layer(round_that_ends_with(s - LAG_QUANTISE_Y))
-            if s < ROW_TILES:
-                scale_and_flip(s, centred)
-            if s + STATS_LEAD < ROW_TILES:
-                finish_statistics(s + STATS_LEAD)
-            if round_that_ends_with(s - LAG_REGROUP_H) is not None:
-                regroup_h(round_that_ends_with(s - LAG_REGROUP_H))
-            if round_that_ends_with(s - LAG_GATE) is not None:
-                gate_layer(round_that_ends_with(s - LAG_GATE))
+        flip_layer(0)
+        for k in range(ROUNDS + LAG_GATE):
+            if k < ROUNDS and k % STATS_GROUP == 0:
+                for n in range(k, k + STATS_GROUP):
+                    statistics(n)
+            if k == 0:
+                flip_layer(1)
+            if k < ROUNDS:
+                layer_norm(k)
+            if 0 <= k - LAG_GATE:
+                regroup_h(k - LAG_GATE)
+                quantise_h(k - LAG_GATE)
+                gate_layer(k - LAG_GATE)
+            if 0 <= k - LAG_HIDDEN < ROUNDS:
+                regroup_y(k - LAG_HIDDEN)
+                quantise_y(k - LAG_HIDDEN)
+                hidden_layer(k - LAG_HIDDEN)
+            if k + 1 == LAG_HIDDEN:
+                quantise_layer(0)
+            if k + 1 == LAG_GATE:
+                quantise_layer(1)
+        for n in range(ROUNDS):
+            gated_output(n)

@@ -41,7 +41,7 @@ FLOPS = 2 * ROWS * FEAT * HID * 2
 STATS_GROUP = 2
 LAG_HIDDEN = 2
 LAG_GATE = 4
-RESULT_TILES = 6
+RESULT_TILES = 10
 
 
 def tile_kanlayer_pb_kernel(tc, kan_sum, ln_gamma, ln_beta, se_w1, se_b1, se_w2, se_b2, out):
@@ -57,14 +57,12 @@ def tile_kanlayer_pb_kernel(tc, kan_sum, ln_gamma, ln_beta, se_w1, se_b1, se_w2,
         w1_raw = keep.tile([P, HID_BLOCKS, FEAT], BF16)
         w2_raw = keep.tile([P, FEAT_BLOCKS, HID], BF16)
         z_tiles = kan_sum.rearrange("(i p) f -> p i f", p=P)
-        for i in range(ROUND_TILES):
+        for i in range(STATS_GROUP * ROUND_TILES):
             nc.sync.dma_start(out=z_all[:, i, :], in_=z_tiles[:, i, :])
         nc.sync.dma_start(
             out=w1_raw[:].rearrange("q (a e) f -> q a e f", e=PAIR),
             in_=se_w1.rearrange("(a q e) f -> q a e f", q=P, e=PAIR),
         )
-        for i in range(ROUND_TILES, STATS_GROUP * ROUND_TILES):
-            nc.sync.dma_start(out=z_all[:, i, :], in_=z_tiles[:, i, :])
         nc.sync.dma_start(
             out=w2_raw[:].rearrange("q (a e) h -> q a e h", e=PAIR),
             in_=se_w2.rearrange("(a q e) h -> q a e h", q=P, e=PAIR),
@@ -267,17 +265,20 @@ def tile_kanlayer_pb_kernel(tc, kan_sum, ln_gamma, ln_beta, se_w1, se_b1, se_w2,
         def gated_output(n):
             for i in tiles_of(n):
                 rows = slice(i * P, (i + 1) * P)
-                nc.vector.tensor_tensor(out=gate_t[:, :, rows], in0=gate_t[:, :, rows], in1=y_t[:, :, rows], op=ALU.mult)
-                result = work.tile([P, FEAT], F32, bufs=RESULT_TILES)
                 for b in range(FEAT_BANKS):
+                    blocks = slice(b * PACK, (b + 1) * PACK)
+                    nc.vector.tensor_tensor(
+                        out=gate_t[:, blocks, rows], in0=gate_t[:, blocks, rows], in1=y_t[:, blocks, rows], op=ALU.mult
+                    )
                     back = flip.tile([P, PACK, P], F32, tag="flip")
                     for g in range(PACK):
                         nc.tensor.transpose(back[:, g, :], gate_t[:, b * PACK + g, rows], ident[:])
+                    result = work.tile([P, BANK], F32, bufs=RESULT_TILES)
                     nc.scalar.copy(
-                        out=result[:, b * BANK : (b + 1) * BANK].rearrange("p (a q e) -> p a q e", q=P, e=PAIR),
+                        out=result[:].rearrange("p (a q e) -> p a q e", q=P, e=PAIR),
                         in_=back[:].rearrange("p (a e) q -> p a q e", e=PAIR),
                     )
-                nc.sync.dma_start(out=out[rows, :], in_=result[:])
+                    nc.sync.dma_start(out=out[rows, b * BANK : (b + 1) * BANK], in_=result[:])
 
         flip_layer(0)
         for k in range(ROUNDS + LAG_GATE):

@@ -40,7 +40,7 @@ FLOPS = 2 * ROWS * FEAT * HID * 2
 
 STATS_GROUP = 2
 LAG_HIDDEN = 2
-LAG_GATE = 4
+LAG_GATE = 3
 RESULT_TILES = 10
 
 
@@ -50,7 +50,7 @@ def tile_kanlayer_pb_kernel(tc, kan_sum, ln_gamma, ln_beta, se_w1, se_b1, se_w2,
         keep = stack.enter_context(tc.tile_pool(name="keep", bufs=1))
         work = stack.enter_context(tc.tile_pool(name="work", bufs=2 * ROUND_TILES))
         flip = stack.enter_context(tc.psum_pool(name="flip", bufs=4))
-        sums = stack.enter_context(tc.psum_pool(name="sums", bufs=4))
+        sums = stack.enter_context(tc.psum_pool(name="sums", bufs=2))
         stack.enter_context(tc.manual_schedule())
 
         z_all = keep.tile([P, ROW_TILES, FEAT], BF16)
@@ -95,7 +95,6 @@ def tile_kanlayer_pb_kernel(tc, kan_sum, ln_gamma, ln_beta, se_w1, se_b1, se_w2,
         y_grouped = keep.tile([P, ROUNDS, FEAT_PASSES, ROUND_ROWS, PACK], BF16, align_bytes=64)
         y_codes = keep.tile([P, ROUNDS, FEAT_PASSES, ROUND_ROWS], U32, align_bytes=64)
         y_scales = keep.tile([P, ROUNDS, FEAT_PASSES, ROUND_ROWS], U8, align_bytes=64)
-        h_planes = keep.tile([P, HID_BLOCKS, ROWS], BF16)
         h_grouped = keep.tile([P, ROWS, PACK], BF16, align_bytes=64)
         h_codes = keep.tile([P, ROWS], U32, align_bytes=64)
         h_scales = keep.tile([P, ROWS], U8, align_bytes=64)
@@ -203,34 +202,39 @@ def tile_kanlayer_pb_kernel(tc, kan_sum, ln_gamma, ln_beta, se_w1, se_b1, se_w2,
                 in_=y_grouped[:, n].rearrange("p c r t -> p (c r t)"),
             )
 
-        def hidden_layer(n):
-            for first in range(0, HID_BLOCKS, PER_BANK):
-                h_sum = sums.tile([P, PER_BANK, ROUND_ROWS], F32, tag="sums")
-                for g in range(PER_BANK):
+        def hidden_sums(n):
+            h_sums = []
+            for a in range(ROUND_TILES):
+                h_sum = sums.tile([P, HID_BLOCKS, P], F32, tag="h_sum")
+                for m in range(HID_BLOCKS):
                     for c in range(FEAT_PASSES):
-                        units = slice((c * HID_BLOCKS + first + g) * P, (c * HID_BLOCKS + first + g + 1) * P)
+                        units = slice((c * HID_BLOCKS + m) * P, (c * HID_BLOCKS + m + 1) * P)
+                        rows = slice(a * P, (a + 1) * P)
                         nc.tensor.matmul_mx(
-                            out=h_sum[:, g, :],
+                            out=h_sum[:, m, :],
                             lhsT=w_codes[:, units].bitcast(FP8X4),
                             lhsT_scale=w_scales[:, units],
-                            rhs=y_codes[:, n, c, :].bitcast(FP8X4),
-                            rhs_scale=y_scales[:, n, c, :],
+                            rhs=y_codes[:, n, c, rows].bitcast(FP8X4),
+                            rhs_scale=y_scales[:, n, c, rows],
                             start=(c == 0),
                             stop=(c == FEAT_PASSES - 1),
                         )
-                for g in range(PER_BANK):
-                    m = first + g
-                    nc.scalar.activation(
-                        out=h_planes[:, m, rows_of(n)],
-                        in_=h_sum[:, g, :],
-                        func=ACT.Relu,
-                        bias=vec_cols[:, B1 + m : B1 + m + 1],
-                    )
+                h_sums.append(h_sum)
+            return h_sums
 
-        def regroup_h(n):
-            nc.vector.tensor_copy(
-                out=h_grouped[:, rows_of(n), :], in_=h_planes[:, :, rows_of(n)].rearrange("p m r -> p r m")
-            )
+        def hidden_bias(n, h_sums):
+            b1_words = vec_cols[:, B1 : B1 + HID_BLOCKS].unsqueeze(1).to_broadcast([P, P, HID_BLOCKS])
+            for i, h_sum in zip(tiles_of(n), h_sums):
+                nc.vector.tensor_tensor(
+                    out=h_grouped[:, i * P : (i + 1) * P, :],
+                    in0=h_sum[:].rearrange("p m r -> p r m"),
+                    in1=b1_words,
+                    op=ALU.add,
+                )
+
+        def hidden_relu(n):
+            h = h_grouped[:, rows_of(n), :].rearrange("p r m -> p (r m)")
+            nc.vector.tensor_scalar_max(out=h, in0=h, scalar1=0.0)
 
         def quantise_h(n):
             nc.vector.quantize_mx(
@@ -241,7 +245,7 @@ def tile_kanlayer_pb_kernel(tc, kan_sum, ln_gamma, ln_beta, se_w1, se_b1, se_w2,
 
         def gate_layer(n):
             for first in range(0, FEAT_BLOCKS, PER_BANK):
-                g_sum = sums.tile([P, PER_BANK, ROUND_ROWS], F32, tag="sums")
+                g_sum = sums.tile([P, PER_BANK, ROUND_ROWS], F32, tag="g_sum")
                 for g in range(PER_BANK):
                     feats = slice(LAYER_WORDS + (first + g) * P, LAYER_WORDS + (first + g + 1) * P)
                     nc.tensor.matmul_mx(
@@ -281,7 +285,10 @@ def tile_kanlayer_pb_kernel(tc, kan_sum, ln_gamma, ln_beta, se_w1, se_b1, se_w2,
                     nc.sync.dma_start(out=out[rows, b * BANK : (b + 1) * BANK], in_=result[:])
 
         flip_layer(0)
+        h_sums = {}
         for k in range(ROUNDS + LAG_GATE):
+            y_round, h_round = k - LAG_HIDDEN, k - LAG_GATE
+            take_y, take_h = 0 <= y_round < ROUNDS, 0 <= h_round < ROUNDS
             if k < ROUNDS and k % STATS_GROUP == 0:
                 for n in range(k, k + STATS_GROUP):
                     statistics(n)
@@ -289,14 +296,18 @@ def tile_kanlayer_pb_kernel(tc, kan_sum, ln_gamma, ln_beta, se_w1, se_b1, se_w2,
                 flip_layer(1)
             if k < ROUNDS:
                 layer_norm(k)
-            if 0 <= k - LAG_GATE:
-                regroup_h(k - LAG_GATE)
-                quantise_h(k - LAG_GATE)
-                gate_layer(k - LAG_GATE)
-            if 0 <= k - LAG_HIDDEN < ROUNDS:
-                regroup_y(k - LAG_HIDDEN)
-                quantise_y(k - LAG_HIDDEN)
-                hidden_layer(k - LAG_HIDDEN)
+            if take_h:
+                hidden_bias(h_round, h_sums[h_round])
+            if take_y:
+                regroup_y(y_round)
+            if take_h:
+                hidden_relu(h_round)
+            if take_y:
+                quantise_y(y_round)
+                h_sums[y_round] = hidden_sums(y_round)
+            if take_h:
+                quantise_h(h_round)
+                gate_layer(h_round)
             if k + 1 == LAG_HIDDEN:
                 quantise_layer(0)
             if k + 1 == LAG_GATE:

@@ -38,9 +38,10 @@ VEC_COLS = 3 * FEAT_BLOCKS + HID_BLOCKS
 
 FLOPS = 2 * ROWS * FEAT * HID * 2
 
-STATS_GROUP = 2
-LAG_HIDDEN = 2
-LAG_GATE = 3
+GPSIMD_ROUNDS = 4
+NORM_AHEAD = 3
+SHARED_ROUNDS = 2
+FIRST_TILES = 3
 RESULT_TILES = 10
 
 
@@ -48,7 +49,7 @@ def tile_kanlayer_pb_kernel(tc, kan_sum, ln_gamma, ln_beta, se_w1, se_b1, se_w2,
     nc = tc.nc
     with ExitStack() as stack:
         keep = stack.enter_context(tc.tile_pool(name="keep", bufs=1))
-        work = stack.enter_context(tc.tile_pool(name="work", bufs=2 * ROUND_TILES))
+        work = stack.enter_context(tc.tile_pool(name="work", bufs=ROW_TILES))
         flip = stack.enter_context(tc.psum_pool(name="flip", bufs=4))
         sums = stack.enter_context(tc.psum_pool(name="sums", bufs=2))
         stack.enter_context(tc.manual_schedule())
@@ -57,17 +58,19 @@ def tile_kanlayer_pb_kernel(tc, kan_sum, ln_gamma, ln_beta, se_w1, se_b1, se_w2,
         w1_raw = keep.tile([P, HID_BLOCKS, FEAT], BF16)
         w2_raw = keep.tile([P, FEAT_BLOCKS, HID], BF16)
         z_tiles = kan_sum.rearrange("(i p) f -> p i f", p=P)
-        for i in range(STATS_GROUP * ROUND_TILES):
+        for i in range(FIRST_TILES):
             nc.sync.dma_start(out=z_all[:, i, :], in_=z_tiles[:, i, :])
-        nc.sync.dma_start(
-            out=w1_raw[:].rearrange("q (a e) f -> q a e f", e=PAIR),
-            in_=se_w1.rearrange("(a q e) f -> q a e f", q=P, e=PAIR),
-        )
+        for a in range(HID_BLOCKS // PAIR):
+            nc.sync.dma_start(
+                out=w1_raw[:, a * PAIR : (a + 1) * PAIR, :],
+                in_=se_w1.rearrange("(a q e) f -> a q e f", q=P, e=PAIR)[a],
+            )
+        for i in range(FIRST_TILES, ROW_TILES):
+            nc.sync.dma_start(out=z_all[:, i, :], in_=z_tiles[:, i, :])
         nc.sync.dma_start(
             out=w2_raw[:].rearrange("q (a e) h -> q a e h", e=PAIR),
             in_=se_w2.rearrange("(a q e) h -> q a e h", q=P, e=PAIR),
         )
-        nc.sync.dma_start(out=z_all[:, STATS_GROUP * ROUND_TILES :, :], in_=z_tiles[:, STATS_GROUP * ROUND_TILES :, :])
 
         vec_rows = keep.tile([P, PAIR * P], BF16)
         nc.vector.memset(vec_rows[:], 0.0)
@@ -76,17 +79,19 @@ def tile_kanlayer_pb_kernel(tc, kan_sum, ln_gamma, ln_beta, se_w1, se_b1, se_w2,
             first_row = first_col // PAIR
             nc.scalar.dma_start(out=vec_rows[first_row : first_row + rows_of_vec.shape[0], :], in_=rows_of_vec)
 
-        minus_half = keep.tile([P, 1], F32)
+        minus_half = keep.tile([P, ROUND_TILES], F32)
         nc.gpsimd.memset(minus_half[:], -0.5)
         ident = keep.tile([P, P], F32)
         make_identity(nc, ident[:])
         table_warmer = keep.tile([P, 1], F32)
-        nc.scalar.activation(out=table_warmer[:], in_=minus_half[:], func=ACT.Sigmoid)
+        nc.scalar.activation(out=table_warmer[:], in_=minus_half[:, 0:1], func=ACT.Sigmoid)
 
-        vec_flip = flip.tile([P, P], F32, tag="flip")
-        nc.tensor.transpose(vec_flip[:], vec_rows[:].bitcast(F32), ident[:])
         vec_cols = keep.tile([P, VEC_COLS], F32)
-        nc.scalar.copy(out=vec_cols[:], in_=vec_flip[:].bitcast(BF16)[:, 0:VEC_COLS])
+
+        def flip_vectors():
+            vec_flip = flip.tile([P, P], F32, tag="flip")
+            nc.tensor.transpose(vec_flip[:], vec_rows[:].bitcast(F32), ident[:])
+            nc.scalar.copy(out=vec_cols[:], in_=vec_flip[:].bitcast(BF16)[:, 0:VEC_COLS])
 
         w_grouped = keep.tile([P, LAYERS * LAYER_WORDS * PACK], BF16, align_bytes=64)
         w_codes = keep.tile([P, LAYERS * LAYER_WORDS], U32, align_bytes=64)
@@ -103,6 +108,7 @@ def tile_kanlayer_pb_kernel(tc, kan_sum, ln_gamma, ln_beta, se_w1, se_b1, se_w2,
         mean_var = keep.tile([P, ROW_TILES, 2], F32)
         var_eps = keep.tile([P, ROW_TILES], F32)
         rstd = keep.tile([P, ROW_TILES], F32)
+        shift = keep.tile([P, ROW_TILES], F32)
 
         w_grouped_words = w_grouped[:].bitcast(F32).rearrange("p (r u) -> p r u", u=PAIR)
         w1_words = w1_raw[:].rearrange("q m f -> q (m f)").bitcast(F32).rearrange("q (m w) -> q m w", m=HID_BLOCKS)
@@ -145,41 +151,52 @@ def tile_kanlayer_pb_kernel(tc, kan_sum, ln_gamma, ln_beta, se_w1, se_b1, se_w2,
         def rows_of(n):
             return slice(n * ROUND_ROWS, (n + 1) * ROUND_ROWS)
 
-        def statistics(n):
+        def statistics(i):
+            for b in range(FEAT_BANKS):
+                nc.vector.bn_stats(out=stats[:, i, b, :], in_=z_all[:, i, b * BANK : (b + 1) * BANK])
+            nc.vector.bn_aggr(out=mean_var[:, i, :], in_=stats[:, i, :, :].rearrange("p b d -> p (b d)"))
+
+        def reciprocal_deviation(n):
+            tiles = slice(n * ROUND_TILES, (n + 1) * ROUND_TILES)
+            nc.gpsimd.tensor_scalar(
+                out=var_eps[:, tiles],
+                in0=mean_var[:, tiles, 1],
+                scalar1=1.0,
+                scalar2=LN_EPS,
+                op0=ALU.mult,
+                op1=ALU.add,
+            )
+            nc.gpsimd.tensor_tensor(out=rstd[:, tiles], in0=var_eps[:, tiles], in1=minus_half[:], op=ALU.pow)
+            nc.gpsimd.tensor_scalar(
+                out=var_eps[:, tiles],
+                in0=mean_var[:, tiles, 0],
+                scalar1=-1.0,
+                scalar2=0.0,
+                op0=ALU.mult,
+                op1=ALU.add,
+            )
+            nc.gpsimd.tensor_tensor(out=shift[:, tiles], in0=var_eps[:, tiles], in1=rstd[:, tiles], op=ALU.mult)
+
+        def normalise(n):
+            engine = nc.gpsimd if n < GPSIMD_ROUNDS else nc.vector
             for i in tiles_of(n):
-                for b in range(FEAT_BANKS):
-                    nc.vector.bn_stats(out=stats[:, i, b, :], in_=z_all[:, i, b * BANK : (b + 1) * BANK])
-            for i in tiles_of(n):
-                nc.vector.bn_aggr(out=mean_var[:, i, :], in_=stats[:, i, :, :].rearrange("p b d -> p (b d)"))
-                nc.gpsimd.tensor_scalar(
-                    out=var_eps[:, i : i + 1],
-                    in0=mean_var[:, i, 1:2],
-                    scalar1=1.0,
-                    scalar2=LN_EPS,
+                xhat = work.tile([P, FEAT_BLOCKS, P], F32)
+                engine.tensor_scalar(
+                    out=xhat[:].rearrange("p (a e) q -> p a e q", e=PAIR),
+                    in0=z_all[:, i, :].rearrange("p (a q e) -> p a e q", q=P, e=PAIR),
+                    scalar1=rstd[:, i : i + 1],
+                    scalar2=shift[:, i : i + 1],
                     op0=ALU.mult,
                     op1=ALU.add,
                 )
-                nc.gpsimd.tensor_tensor(out=rstd[:, i : i + 1], in0=var_eps[:, i : i + 1], in1=minus_half[:], op=ALU.pow)
+                xhats[i] = xhat
 
-        def normalise(i):
-            xhat = work.tile([P, FEAT_BLOCKS, P], F32)
-            nc.vector.tensor_scalar(
-                out=xhat[:].rearrange("p (a e) q -> p a e q", e=PAIR),
-                in0=z_all[:, i, :].rearrange("p (a q e) -> p a e q", q=P, e=PAIR),
-                scalar1=mean_var[:, i, 0:1],
-                scalar2=rstd[:, i : i + 1],
-                op0=ALU.subtract,
-                op1=ALU.mult,
-            )
-            return xhat
-
-        def layer_norm(n):
-            xhats = [normalise(i) for i in tiles_of(n)]
+        def affine(n):
             for first in range(0, FEAT_BLOCKS, PER_BANK):
                 flipped = flip.tile([P, PER_BANK, ROUND_ROWS], F32, tag="flip")
                 for g in range(PER_BANK):
-                    for a in range(ROUND_TILES):
-                        nc.tensor.transpose(flipped[:, g, a * P : (a + 1) * P], xhats[a][:, first + g, :], ident[:])
+                    for a, i in enumerate(tiles_of(n)):
+                        nc.tensor.transpose(flipped[:, g, a * P : (a + 1) * P], xhats[i][:, first + g, :], ident[:])
                 for g in range(PER_BANK):
                     j = first + g
                     nc.scalar.activation(
@@ -266,51 +283,79 @@ def tile_kanlayer_pb_kernel(tc, kan_sum, ln_gamma, ln_beta, se_w1, se_b1, se_w2,
                         bias=vec_cols[:, B2 + j : B2 + j + 1],
                     )
 
-        def gated_output(n):
-            for i in tiles_of(n):
-                rows = slice(i * P, (i + 1) * P)
-                for b in range(FEAT_BANKS):
-                    blocks = slice(b * PACK, (b + 1) * PACK)
-                    nc.vector.tensor_tensor(
-                        out=gate_t[:, blocks, rows], in0=gate_t[:, blocks, rows], in1=y_t[:, blocks, rows], op=ALU.mult
-                    )
-                    back = flip.tile([P, PACK, P], F32, tag="flip")
-                    for g in range(PACK):
-                        nc.tensor.transpose(back[:, g, :], gate_t[:, b * PACK + g, rows], ident[:])
-                    result = work.tile([P, BANK], F32, bufs=RESULT_TILES)
-                    nc.scalar.copy(
-                        out=result[:].rearrange("p (a q e) -> p a q e", q=P, e=PAIR),
-                        in_=back[:].rearrange("p (a e) q -> p a q e", e=PAIR),
-                    )
-                    nc.sync.dma_start(out=out[rows, b * BANK : (b + 1) * BANK], in_=result[:])
+        def chunks_of(n):
+            return [(i, b) for b in range(FEAT_BANKS) for i in tiles_of(n)]
 
-        flip_layer(0)
+        def product(i, b):
+            rows = slice(i * P, (i + 1) * P)
+            blocks = slice(b * PACK, (b + 1) * PACK)
+            nc.vector.tensor_tensor(
+                out=gate_t[:, blocks, rows], in0=gate_t[:, blocks, rows], in1=y_t[:, blocks, rows], op=ALU.mult
+            )
+
+        def store(i, b, copy):
+            rows = slice(i * P, (i + 1) * P)
+            back = flip.tile([P, PACK, P], F32, tag="flip")
+            for g in range(PACK):
+                nc.tensor.transpose(back[:, g, :], gate_t[:, b * PACK + g, rows], ident[:])
+            result = work.tile([P, BANK], F32, bufs=RESULT_TILES)
+            copy(
+                out=result[:].rearrange("p (a q e) -> p a q e", q=P, e=PAIR),
+                in_=back[:].rearrange("p (a e) q -> p a q e", e=PAIR),
+            )
+            nc.sync.dma_start(out=out[rows, b * BANK : (b + 1) * BANK], in_=result[:])
+
+        xhats = {}
         h_sums = {}
-        for k in range(ROUNDS + LAG_GATE):
-            y_round, h_round = k - LAG_HIDDEN, k - LAG_GATE
-            take_y, take_h = 0 <= y_round < ROUNDS, 0 <= h_round < ROUNDS
-            if k < ROUNDS and k % STATS_GROUP == 0:
-                for n in range(k, k + STATS_GROUP):
-                    statistics(n)
-            if k == 0:
-                flip_layer(1)
-            if k < ROUNDS:
-                layer_norm(k)
-            if take_h:
-                hidden_bias(h_round, h_sums[h_round])
-            if take_y:
-                regroup_y(y_round)
-            if take_h:
-                hidden_relu(h_round)
-            if take_y:
-                quantise_y(y_round)
-                h_sums[y_round] = hidden_sums(y_round)
-            if take_h:
-                quantise_h(h_round)
-                gate_layer(h_round)
-            if k + 1 == LAG_HIDDEN:
-                quantise_layer(0)
-            if k + 1 == LAG_GATE:
-                quantise_layer(1)
+        flip_layer(0)
+        flip_vectors()
         for n in range(ROUNDS):
-            gated_output(n)
+            for i in tiles_of(n):
+                statistics(i)
+            reciprocal_deviation(n)
+            if n < GPSIMD_ROUNDS:
+                normalise(n)
+            if n - 1 >= GPSIMD_ROUNDS:
+                normalise(n - 1)
+        quantise_layer(0)
+        if ROUNDS > GPSIMD_ROUNDS:
+            normalise(ROUNDS - 1)
+        affine(0)
+        flip_layer(1)
+        for n in range(1, NORM_AHEAD):
+            affine(n)
+        for n in range(ROUNDS):
+            regroup_y(n)
+            if n >= 1:
+                hidden_bias(n - 1, h_sums[n - 1])
+            quantise_y(n)
+            h_sums[n] = hidden_sums(n)
+            if n + NORM_AHEAD < ROUNDS:
+                affine(n + NORM_AHEAD)
+            if n >= 1:
+                hidden_relu(n - 1)
+                quantise_h(n - 1)
+                gate_layer(n - 1)
+            else:
+                quantise_layer(1)
+        last = ROUNDS - 1
+        first_chunks = chunks_of(0)
+        product(*first_chunks[0])
+        product(*first_chunks[1])
+        hidden_bias(last, h_sums[last])
+        product(*first_chunks[2])
+        hidden_relu(last)
+        product(*first_chunks[3])
+        quantise_h(last)
+        for i, b in first_chunks:
+            store(i, b, nc.scalar.copy)
+        gate_layer(last)
+        for n in range(1, ROUNDS - SHARED_ROUNDS):
+            for i, b in chunks_of(n):
+                product(i, b)
+                store(i, b, nc.scalar.copy)
+        shared = [chunk for n in range(ROUNDS - SHARED_ROUNDS, ROUNDS) for chunk in chunks_of(n)]
+        for i, b in shared:
+            product(i, b)
+        for place, (i, b) in enumerate(shared):
+            store(i, b, nc.vector.tensor_copy if place % 2 else nc.scalar.copy)

@@ -38,9 +38,10 @@ VEC_COLS = 3 * FEAT_BLOCKS + HID_BLOCKS
 
 FLOPS = 2 * ROWS * FEAT * HID * 2
 
-GPSIMD_ROUNDS = 4
-NORM_AHEAD = 3
-SHARED_ROUNDS = 2
+LAG_HIDDEN = 1
+LAG_GATE = 2
+LAG_PRODUCT = 3
+GPSIMD_TILES = (0, 2, 3, 4, 6, 7)
 FIRST_TILES = 3
 RESULT_TILES = 10
 
@@ -51,7 +52,7 @@ def tile_kanlayer_pb_kernel(tc, kan_sum, ln_gamma, ln_beta, se_w1, se_b1, se_w2,
         keep = stack.enter_context(tc.tile_pool(name="keep", bufs=1))
         work = stack.enter_context(tc.tile_pool(name="work", bufs=ROW_TILES))
         flip = stack.enter_context(tc.psum_pool(name="flip", bufs=4))
-        sums = stack.enter_context(tc.psum_pool(name="sums", bufs=2))
+        sums = stack.enter_context(tc.psum_pool(name="sums", bufs=4))
         stack.enter_context(tc.manual_schedule())
 
         z_all = keep.tile([P, ROW_TILES, FEAT], BF16)
@@ -65,7 +66,8 @@ def tile_kanlayer_pb_kernel(tc, kan_sum, ln_gamma, ln_beta, se_w1, se_b1, se_w2,
                 out=w1_raw[:, a * PAIR : (a + 1) * PAIR, :],
                 in_=se_w1.rearrange("(a q e) f -> a q e f", q=P, e=PAIR)[a],
             )
-        for i in range(FIRST_TILES, ROW_TILES):
+            nc.sync.dma_start(out=z_all[:, FIRST_TILES + a, :], in_=z_tiles[:, FIRST_TILES + a, :])
+        for i in range(FIRST_TILES + HID_BLOCKS // PAIR, ROW_TILES):
             nc.sync.dma_start(out=z_all[:, i, :], in_=z_tiles[:, i, :])
         nc.sync.dma_start(
             out=w2_raw[:].rearrange("q (a e) h -> q a e h", e=PAIR),
@@ -100,6 +102,7 @@ def tile_kanlayer_pb_kernel(tc, kan_sum, ln_gamma, ln_beta, se_w1, se_b1, se_w2,
         y_grouped = keep.tile([P, ROUNDS, FEAT_PASSES, ROUND_ROWS, PACK], BF16, align_bytes=64)
         y_codes = keep.tile([P, ROUNDS, FEAT_PASSES, ROUND_ROWS], U32, align_bytes=64)
         y_scales = keep.tile([P, ROUNDS, FEAT_PASSES, ROUND_ROWS], U8, align_bytes=64)
+        h_planes = keep.tile([P, HID_BLOCKS, ROWS], BF16)
         h_grouped = keep.tile([P, ROWS, PACK], BF16, align_bytes=64)
         h_codes = keep.tile([P, ROWS], U32, align_bytes=64)
         h_scales = keep.tile([P, ROWS], U8, align_bytes=64)
@@ -154,6 +157,8 @@ def tile_kanlayer_pb_kernel(tc, kan_sum, ln_gamma, ln_beta, se_w1, se_b1, se_w2,
         def statistics(i):
             for b in range(FEAT_BANKS):
                 nc.vector.bn_stats(out=stats[:, i, b, :], in_=z_all[:, i, b * BANK : (b + 1) * BANK])
+
+        def aggregate(i):
             nc.vector.bn_aggr(out=mean_var[:, i, :], in_=stats[:, i, :, :].rearrange("p b d -> p (b d)"))
 
         def reciprocal_deviation(n):
@@ -177,19 +182,29 @@ def tile_kanlayer_pb_kernel(tc, kan_sum, ln_gamma, ln_beta, se_w1, se_b1, se_w2,
             )
             nc.gpsimd.tensor_tensor(out=shift[:, tiles], in0=var_eps[:, tiles], in1=rstd[:, tiles], op=ALU.mult)
 
-        def normalise(n):
-            engine = nc.gpsimd if n < GPSIMD_ROUNDS else nc.vector
-            for i in tiles_of(n):
-                xhat = work.tile([P, FEAT_BLOCKS, P], F32)
-                engine.tensor_scalar(
-                    out=xhat[:].rearrange("p (a e) q -> p a e q", e=PAIR),
-                    in0=z_all[:, i, :].rearrange("p (a q e) -> p a e q", q=P, e=PAIR),
+        def normalise(i):
+            xhat = work.tile([P, FEAT_BLOCKS, P], F32)
+            xhats[i] = xhat
+            sorted_out = xhat[:].rearrange("p (a e) q -> p a e q", e=PAIR)
+            z_in = z_all[:, i, :].rearrange("p (a q e) -> p a e q", q=P, e=PAIR)
+            if i in GPSIMD_TILES:
+                nc.gpsimd.tensor_scalar(
+                    out=sorted_out,
+                    in0=z_in,
                     scalar1=rstd[:, i : i + 1],
                     scalar2=shift[:, i : i + 1],
                     op0=ALU.mult,
                     op1=ALU.add,
                 )
-                xhats[i] = xhat
+            else:
+                nc.vector.tensor_scalar(
+                    out=sorted_out,
+                    in0=z_in,
+                    scalar1=mean_var[:, i, 0:1],
+                    scalar2=rstd[:, i : i + 1],
+                    op0=ALU.subtract,
+                    op1=ALU.mult,
+                )
 
         def affine(n):
             for first in range(0, FEAT_BLOCKS, PER_BANK):
@@ -219,39 +234,34 @@ def tile_kanlayer_pb_kernel(tc, kan_sum, ln_gamma, ln_beta, se_w1, se_b1, se_w2,
                 in_=y_grouped[:, n].rearrange("p c r t -> p (c r t)"),
             )
 
-        def hidden_sums(n):
-            h_sums = []
-            for a in range(ROUND_TILES):
-                h_sum = sums.tile([P, HID_BLOCKS, P], F32, tag="h_sum")
-                for m in range(HID_BLOCKS):
+        def hidden_layer(n):
+            for first in range(0, HID_BLOCKS, PER_BANK):
+                h_sum = sums.tile([P, PER_BANK, ROUND_ROWS], F32, tag="sums")
+                for g in range(PER_BANK):
                     for c in range(FEAT_PASSES):
-                        units = slice((c * HID_BLOCKS + m) * P, (c * HID_BLOCKS + m + 1) * P)
-                        rows = slice(a * P, (a + 1) * P)
+                        units = slice((c * HID_BLOCKS + first + g) * P, (c * HID_BLOCKS + first + g + 1) * P)
                         nc.tensor.matmul_mx(
-                            out=h_sum[:, m, :],
+                            out=h_sum[:, g, :],
                             lhsT=w_codes[:, units].bitcast(FP8X4),
                             lhsT_scale=w_scales[:, units],
-                            rhs=y_codes[:, n, c, rows].bitcast(FP8X4),
-                            rhs_scale=y_scales[:, n, c, rows],
+                            rhs=y_codes[:, n, c, :].bitcast(FP8X4),
+                            rhs_scale=y_scales[:, n, c, :],
                             start=(c == 0),
                             stop=(c == FEAT_PASSES - 1),
                         )
-                h_sums.append(h_sum)
-            return h_sums
+                for g in range(PER_BANK):
+                    m = first + g
+                    nc.scalar.activation(
+                        out=h_planes[:, m, rows_of(n)],
+                        in_=h_sum[:, g, :],
+                        func=ACT.Relu,
+                        bias=vec_cols[:, B1 + m : B1 + m + 1],
+                    )
 
-        def hidden_bias(n, h_sums):
-            b1_words = vec_cols[:, B1 : B1 + HID_BLOCKS].unsqueeze(1).to_broadcast([P, P, HID_BLOCKS])
-            for i, h_sum in zip(tiles_of(n), h_sums):
-                nc.vector.tensor_tensor(
-                    out=h_grouped[:, i * P : (i + 1) * P, :],
-                    in0=h_sum[:].rearrange("p m r -> p r m"),
-                    in1=b1_words,
-                    op=ALU.add,
-                )
-
-        def hidden_relu(n):
-            h = h_grouped[:, rows_of(n), :].rearrange("p r m -> p (r m)")
-            nc.vector.tensor_scalar_max(out=h, in0=h, scalar1=0.0)
+        def regroup_h(n):
+            nc.vector.tensor_copy(
+                out=h_grouped[:, rows_of(n), :], in_=h_planes[:, :, rows_of(n)].rearrange("p m r -> p r m")
+            )
 
         def quantise_h(n):
             nc.vector.quantize_mx(
@@ -262,7 +272,7 @@ def tile_kanlayer_pb_kernel(tc, kan_sum, ln_gamma, ln_beta, se_w1, se_b1, se_w2,
 
         def gate_layer(n):
             for first in range(0, FEAT_BLOCKS, PER_BANK):
-                g_sum = sums.tile([P, PER_BANK, ROUND_ROWS], F32, tag="g_sum")
+                g_sum = sums.tile([P, PER_BANK, ROUND_ROWS], F32, tag="sums")
                 for g in range(PER_BANK):
                     feats = slice(LAYER_WORDS + (first + g) * P, LAYER_WORDS + (first + g + 1) * P)
                     nc.tensor.matmul_mx(
@@ -283,79 +293,83 @@ def tile_kanlayer_pb_kernel(tc, kan_sum, ln_gamma, ln_beta, se_w1, se_b1, se_w2,
                         bias=vec_cols[:, B2 + j : B2 + j + 1],
                     )
 
-        def chunks_of(n):
-            return [(i, b) for b in range(FEAT_BANKS) for i in tiles_of(n)]
+        def products(n):
+            for b in range(FEAT_BANKS):
+                blocks = slice(b * PACK, (b + 1) * PACK)
+                nc.vector.tensor_tensor(
+                    out=gate_t[:, blocks, rows_of(n)],
+                    in0=gate_t[:, blocks, rows_of(n)],
+                    in1=y_t[:, blocks, rows_of(n)],
+                    op=ALU.mult,
+                )
 
-        def product(i, b):
-            rows = slice(i * P, (i + 1) * P)
-            blocks = slice(b * PACK, (b + 1) * PACK)
-            nc.vector.tensor_tensor(
-                out=gate_t[:, blocks, rows], in0=gate_t[:, blocks, rows], in1=y_t[:, blocks, rows], op=ALU.mult
-            )
-
-        def store(i, b, copy):
+        def flip_back(i, b):
             rows = slice(i * P, (i + 1) * P)
             back = flip.tile([P, PACK, P], F32, tag="flip")
             for g in range(PACK):
                 nc.tensor.transpose(back[:, g, :], gate_t[:, b * PACK + g, rows], ident[:])
+            return back
+
+        def store(i, b, back, copy):
             result = work.tile([P, BANK], F32, bufs=RESULT_TILES)
             copy(
                 out=result[:].rearrange("p (a q e) -> p a q e", q=P, e=PAIR),
                 in_=back[:].rearrange("p (a e) q -> p a q e", e=PAIR),
             )
-            nc.sync.dma_start(out=out[rows, b * BANK : (b + 1) * BANK], in_=result[:])
+            nc.sync.dma_start(out=out[i * P : (i + 1) * P, b * BANK : (b + 1) * BANK], in_=result[:])
+
+        def vector_store():
+            for i, b, back in left_over:
+                store(i, b, back, nc.vector.tensor_copy)
+            left_over.clear()
+
+        def stores(n, b):
+            vector_store()
+            first, second = tiles_of(n)
+            store(first, b, flip_back(first, b), nc.scalar.copy)
+            left_over.append((second, b, flip_back(second, b)))
 
         xhats = {}
-        h_sums = {}
+        left_over = []
         flip_layer(0)
         flip_vectors()
-        for n in range(ROUNDS):
-            for i in tiles_of(n):
-                statistics(i)
-            reciprocal_deviation(n)
-            if n < GPSIMD_ROUNDS:
-                normalise(n)
-            if n - 1 >= GPSIMD_ROUNDS:
-                normalise(n - 1)
-        quantise_layer(0)
-        if ROUNDS > GPSIMD_ROUNDS:
-            normalise(ROUNDS - 1)
-        affine(0)
-        flip_layer(1)
-        for n in range(1, NORM_AHEAD):
-            affine(n)
-        for n in range(ROUNDS):
-            regroup_y(n)
-            if n >= 1:
-                hidden_bias(n - 1, h_sums[n - 1])
-            quantise_y(n)
-            h_sums[n] = hidden_sums(n)
-            if n + NORM_AHEAD < ROUNDS:
-                affine(n + NORM_AHEAD)
-            if n >= 1:
-                hidden_relu(n - 1)
-                quantise_h(n - 1)
-                gate_layer(n - 1)
-            else:
+        for n in range(-1, ROUNDS + LAG_PRODUCT + 1):
+            y_round, h_round, done = n - LAG_HIDDEN, n - LAG_GATE, n - LAG_PRODUCT
+            if n + 1 < ROUNDS:
+                for i in tiles_of(n + 1):
+                    statistics(i)
+            if 0 <= n < ROUNDS:
+                for i in tiles_of(n):
+                    if i not in GPSIMD_TILES:
+                        normalise(i)
+            if n + 1 < ROUNDS:
+                for i in tiles_of(n + 1):
+                    aggregate(i)
+                reciprocal_deviation(n + 1)
+                for i in tiles_of(n + 1):
+                    if i in GPSIMD_TILES:
+                        normalise(i)
+            if 0 <= n < ROUNDS:
+                affine(n)
+            if n == 0:
+                flip_layer(1)
+            if n == LAG_HIDDEN:
+                quantise_layer(0)
+            if 0 <= y_round < ROUNDS:
+                regroup_y(y_round)
+            if 0 <= h_round < ROUNDS:
+                regroup_h(h_round)
+            if 0 <= y_round < ROUNDS:
+                quantise_y(y_round)
+                hidden_layer(y_round)
+            if n == LAG_GATE:
                 quantise_layer(1)
-        last = ROUNDS - 1
-        first_chunks = chunks_of(0)
-        product(*first_chunks[0])
-        product(*first_chunks[1])
-        hidden_bias(last, h_sums[last])
-        product(*first_chunks[2])
-        hidden_relu(last)
-        product(*first_chunks[3])
-        quantise_h(last)
-        for i, b in first_chunks:
-            store(i, b, nc.scalar.copy)
-        gate_layer(last)
-        for n in range(1, ROUNDS - SHARED_ROUNDS):
-            for i, b in chunks_of(n):
-                product(i, b)
-                store(i, b, nc.scalar.copy)
-        shared = [chunk for n in range(ROUNDS - SHARED_ROUNDS, ROUNDS) for chunk in chunks_of(n)]
-        for i, b in shared:
-            product(i, b)
-        for place, (i, b) in enumerate(shared):
-            store(i, b, nc.vector.tensor_copy if place % 2 else nc.scalar.copy)
+            if 0 <= done - 1 < ROUNDS:
+                stores(done - 1, 1)
+            if 0 <= h_round < ROUNDS:
+                quantise_h(h_round)
+                gate_layer(h_round)
+            if 0 <= done < ROUNDS:
+                products(done)
+                stores(done, 0)
+        vector_store()

@@ -41,8 +41,8 @@ FLOPS = 2 * ROWS * FEAT * HID * 2
 LAG_HIDDEN = 1
 LAG_GATE = 2
 LAG_PRODUCT = 3
-GPSIMD_TILES = (0, 2, 3, 4, 6, 7)
-FIRST_TILES = 3
+SCALAR_TILES = (1, 5)
+FIRST_TILES = 2
 RESULT_TILES = 10
 
 
@@ -129,7 +129,10 @@ def tile_kanlayer_pb_kernel(tc, kan_sum, ln_gamma, ln_beta, se_w1, se_b1, se_w2,
 
         def flip_layer(layer):
             blocks = stationary_blocks(layer)
-            for first in range(0, len(blocks), PAIR):
+            pairs = range(0, len(blocks), PAIR)
+            if layer == 0:
+                pairs = sorted(pairs, key=lambda first: first % HID_BLOCKS)
+            for first in pairs:
                 flipped = flip.tile([P, PAIR, PAIR, P], F32, tag="flip")
                 for b in range(PAIR):
                     for u in range(PAIR):
@@ -172,29 +175,32 @@ def tile_kanlayer_pb_kernel(tc, kan_sum, ln_gamma, ln_beta, se_w1, se_b1, se_w2,
                 op1=ALU.add,
             )
             nc.gpsimd.tensor_tensor(out=rstd[:, tiles], in0=var_eps[:, tiles], in1=minus_half[:], op=ALU.pow)
-            nc.gpsimd.tensor_scalar(
-                out=var_eps[:, tiles],
-                in0=mean_var[:, tiles, 0],
-                scalar1=-1.0,
-                scalar2=0.0,
-                op0=ALU.mult,
-                op1=ALU.add,
-            )
-            nc.gpsimd.tensor_tensor(out=shift[:, tiles], in0=var_eps[:, tiles], in1=rstd[:, tiles], op=ALU.mult)
+
+        def shifts(n):
+            for i in tiles_of(n):
+                if i in SCALAR_TILES:
+                    col = slice(i, i + 1)
+                    nc.gpsimd.tensor_scalar(
+                        out=shift[:, col],
+                        in0=mean_var[:, i, 0:1],
+                        scalar1=-1.0,
+                        scalar2=rstd[:, col],
+                        op0=ALU.mult,
+                        op1=ALU.mult,
+                    )
 
         def normalise(i):
             xhat = work.tile([P, FEAT_BLOCKS, P], F32)
             xhats[i] = xhat
             sorted_out = xhat[:].rearrange("p (a e) q -> p a e q", e=PAIR)
             z_in = z_all[:, i, :].rearrange("p (a q e) -> p a e q", q=P, e=PAIR)
-            if i in GPSIMD_TILES:
-                nc.gpsimd.tensor_scalar(
+            if i in SCALAR_TILES:
+                nc.scalar.activation(
                     out=sorted_out,
-                    in0=z_in,
-                    scalar1=rstd[:, i : i + 1],
-                    scalar2=shift[:, i : i + 1],
-                    op0=ALU.mult,
-                    op1=ALU.add,
+                    in_=z_in,
+                    func=ACT.Identity,
+                    scale=rstd[:, i : i + 1],
+                    bias=shift[:, i : i + 1],
                 )
             else:
                 nc.vector.tensor_scalar(
@@ -325,9 +331,12 @@ def tile_kanlayer_pb_kernel(tc, kan_sum, ln_gamma, ln_beta, se_w1, se_b1, se_w2,
 
         def stores(n, b):
             vector_store()
-            first, second = tiles_of(n)
-            store(first, b, flip_back(first, b), nc.scalar.copy)
-            left_over.append((second, b, flip_back(second, b)))
+            for i in tiles_of(n):
+                back = flip_back(i, b)
+                if (i, b) == (n * ROUND_TILES + ROUND_TILES - 1, FEAT_BANKS - 1):
+                    left_over.append((i, b, back))
+                else:
+                    store(i, b, back, nc.scalar.copy)
 
         xhats = {}
         left_over = []
@@ -340,16 +349,17 @@ def tile_kanlayer_pb_kernel(tc, kan_sum, ln_gamma, ln_beta, se_w1, se_b1, se_w2,
                     statistics(i)
             if 0 <= n < ROUNDS:
                 for i in tiles_of(n):
-                    if i not in GPSIMD_TILES:
+                    if i not in SCALAR_TILES:
                         normalise(i)
             if n + 1 < ROUNDS:
                 for i in tiles_of(n + 1):
                     aggregate(i)
                 reciprocal_deviation(n + 1)
-                for i in tiles_of(n + 1):
-                    if i in GPSIMD_TILES:
-                        normalise(i)
+                shifts(n + 1)
             if 0 <= n < ROUNDS:
+                for i in tiles_of(n):
+                    if i in SCALAR_TILES:
+                        normalise(i)
                 affine(n)
             if n == 0:
                 flip_layer(1)

@@ -41,7 +41,8 @@ FLOPS = 2 * ROWS * FEAT * HID * 2
 LAG_HIDDEN = 1
 LAG_GATE = 2
 LAG_PRODUCT = 3
-SCALAR_TILES = (1, 5)
+SCALAR_TILES = (1,)
+GPSIMD_TILES = (2, 4)
 FIRST_TILES = 2
 RESULT_TILES = 10
 
@@ -178,7 +179,7 @@ def tile_kanlayer_pb_kernel(tc, kan_sum, ln_gamma, ln_beta, se_w1, se_b1, se_w2,
 
         def shifts(n):
             for i in tiles_of(n):
-                if i in SCALAR_TILES:
+                if i in SCALAR_TILES + GPSIMD_TILES:
                     col = slice(i, i + 1)
                     nc.gpsimd.tensor_scalar(
                         out=shift[:, col],
@@ -194,7 +195,16 @@ def tile_kanlayer_pb_kernel(tc, kan_sum, ln_gamma, ln_beta, se_w1, se_b1, se_w2,
             xhats[i] = xhat
             sorted_out = xhat[:].rearrange("p (a e) q -> p a e q", e=PAIR)
             z_in = z_all[:, i, :].rearrange("p (a q e) -> p a e q", q=P, e=PAIR)
-            if i in SCALAR_TILES:
+            if i in GPSIMD_TILES:
+                nc.gpsimd.tensor_scalar(
+                    out=sorted_out,
+                    in0=z_in,
+                    scalar1=rstd[:, i : i + 1],
+                    scalar2=shift[:, i : i + 1],
+                    op0=ALU.mult,
+                    op1=ALU.add,
+                )
+            elif i in SCALAR_TILES:
                 nc.scalar.activation(
                     out=sorted_out,
                     in_=z_in,
@@ -333,7 +343,7 @@ def tile_kanlayer_pb_kernel(tc, kan_sum, ln_gamma, ln_beta, se_w1, se_b1, se_w2,
             vector_store()
             for i in tiles_of(n):
                 back = flip_back(i, b)
-                if (i, b) == (n * ROUND_TILES + ROUND_TILES - 1, FEAT_BANKS - 1):
+                if i % ROUND_TILES == 1 and (b == 1 or n % 2 == 1):
                     left_over.append((i, b, back))
                 else:
                     store(i, b, back, nc.scalar.copy)
@@ -349,13 +359,16 @@ def tile_kanlayer_pb_kernel(tc, kan_sum, ln_gamma, ln_beta, se_w1, se_b1, se_w2,
                     statistics(i)
             if 0 <= n < ROUNDS:
                 for i in tiles_of(n):
-                    if i not in SCALAR_TILES:
+                    if i not in SCALAR_TILES + GPSIMD_TILES:
                         normalise(i)
             if n + 1 < ROUNDS:
                 for i in tiles_of(n + 1):
                     aggregate(i)
                 reciprocal_deviation(n + 1)
                 shifts(n + 1)
+                for i in tiles_of(n + 1):
+                    if i in GPSIMD_TILES:
+                        normalise(i)
             if 0 <= n < ROUNDS:
                 for i in tiles_of(n):
                     if i in SCALAR_TILES:

@@ -43,6 +43,7 @@ LAG_GATE = 2
 LAG_PRODUCT = 3
 SCALAR_TILES = (1,)
 GPSIMD_TILES = (2, 4)
+RUN = 4
 FIRST_TILES = 2
 RESULT_TILES = 10
 
@@ -240,7 +241,8 @@ def tile_kanlayer_pb_kernel(tc, kan_sum, ln_gamma, ln_beta, se_w1, se_b1, se_w2,
 
         def regroup_y(n):
             nc.vector.tensor_copy(
-                out=y_grouped[:, n], in_=y_t[:, :, rows_of(n)].rearrange("p (c t) r -> p c r t", t=PACK)
+                out=y_grouped[:, n].rearrange("p c (q i) t -> p c q t i", i=RUN),
+                in_=y_t[:, :, rows_of(n)].rearrange("p (c t) (q i) -> p c q t i", t=PACK, i=RUN),
             )
 
         def quantise_y(n):
@@ -276,7 +278,8 @@ def tile_kanlayer_pb_kernel(tc, kan_sum, ln_gamma, ln_beta, se_w1, se_b1, se_w2,
 
         def regroup_h(n):
             nc.vector.tensor_copy(
-                out=h_grouped[:, rows_of(n), :], in_=h_planes[:, :, rows_of(n)].rearrange("p m r -> p r m")
+                out=h_grouped[:, rows_of(n), :].rearrange("p (q i) m -> p q m i", i=RUN),
+                in_=h_planes[:, :, rows_of(n)].rearrange("p m (q i) -> p q m i", i=RUN),
             )
 
         def quantise_h(n):
@@ -354,13 +357,13 @@ def tile_kanlayer_pb_kernel(tc, kan_sum, ln_gamma, ln_beta, se_w1, se_b1, se_w2,
         flip_vectors()
         for n in range(-1, ROUNDS + LAG_PRODUCT + 1):
             y_round, h_round, done = n - LAG_HIDDEN, n - LAG_GATE, n - LAG_PRODUCT
-            if n + 1 < ROUNDS:
-                for i in tiles_of(n + 1):
-                    statistics(i)
-            if 0 <= n < ROUNDS:
-                for i in tiles_of(n):
-                    if i not in SCALAR_TILES + GPSIMD_TILES:
-                        normalise(i)
+            ahead = list(tiles_of(n + 1)) if n + 1 < ROUNDS else []
+            own = [i for i in tiles_of(n) if i not in SCALAR_TILES + GPSIMD_TILES] if 0 <= n < ROUNDS else []
+            order = [(statistics, i) for i in ahead] + [(normalise, i) for i in own]
+            if n == 0:
+                order[1], order[2] = order[2], order[1]
+            for stage, i in order:
+                stage(i)
             if n + 1 < ROUNDS:
                 for i in tiles_of(n + 1):
                     aggregate(i)

@@ -346,7 +346,7 @@ def tile_kanlayer_pb_kernel(tc, kan_sum, ln_gamma, ln_beta, se_w1, se_b1, se_w2,
             vector_store()
             for i in tiles_of(n):
                 back = flip_back(i, b)
-                if i % ROUND_TILES == 1 and (b == 1 or n % 2 == 1):
+                if i % ROUND_TILES == 1 and (n, b) != (2, 0):
                     left_over.append((i, b, back))
                 else:
                     store(i, b, back, nc.scalar.copy)

from contextlib import ExitStack

import concourse.mybir as mybir
from concourse.masks import make_identity

F32 = mybir.dt.float32
BF16 = mybir.dt.bfloat16
U32 = mybir.dt.uint32
U8 = mybir.dt.uint8
FP8X4 = mybir.dt.float8_e4m3fn_x4
ALU = mybir.AluOpType
ACT = mybir.ActivationFunctionType

P = 128
PACK = 4
PAIR = 2
K_PASS = P * PACK
BANK = 512

ROWS, FEAT, HID = 1024, 1024, 512
LN_EPS = 1e-5
ROW_TILES = ROWS // P
FEAT_BLOCKS = FEAT // P
HID_BLOCKS = HID // P
FEAT_PASSES = FEAT // K_PASS
FEAT_BANKS = FEAT // BANK

ROUND_TILES = 2
ROUND_ROWS = ROUND_TILES * P
ROUNDS = ROW_TILES // ROUND_TILES
PER_BANK = BANK // ROUND_ROWS

LAYERS = 2
LAYER_WORDS = FEAT * HID // K_PASS

GAMMA, BETA, B2, B1 = 0, FEAT_BLOCKS, 2 * FEAT_BLOCKS, 3 * FEAT_BLOCKS
VEC_COLS = 3 * FEAT_BLOCKS + HID_BLOCKS

FLOPS = 2 * ROWS * FEAT * HID * 2

LAG_HIDDEN = 1
LAG_GATE = 2
LAG_PRODUCT = 3
SCALAR_TILES = (1,)
GPSIMD_TILES = (2, 4)
RUN = 4
FIRST_TILES = 2
RESULT_TILES = 10


def tile_kanlayer_pb_kernel(tc, kan_sum, ln_gamma, ln_beta, se_w1, se_b1, se_w2, se_b2, out):
    nc = tc.nc
    with ExitStack() as stack:
        keep = stack.enter_context(tc.tile_pool(name="keep", bufs=1))
        work = stack.enter_context(tc.tile_pool(name="work", bufs=ROW_TILES))
        flip = stack.enter_context(tc.psum_pool(name="flip", bufs=4))
        sums = stack.enter_context(tc.psum_pool(name="sums", bufs=4))
        stack.enter_context(tc.manual_schedule())

        z_all = keep.tile([P, ROW_TILES, FEAT], BF16)
        w1_raw = keep.tile([P, HID_BLOCKS, FEAT], BF16)
        w2_raw = keep.tile([P, FEAT_BLOCKS, HID], BF16)
        z_tiles = kan_sum.rearrange("(i p) f -> p i f", p=P)
        for i in range(FIRST_TILES):
            nc.sync.dma_start(out=z_all[:, i, :], in_=z_tiles[:, i, :])
        for a in range(HID_BLOCKS // PAIR):
            nc.sync.dma_start(
                out=w1_raw[:, a * PAIR : (a + 1) * PAIR, :],
                in_=se_w1.rearrange("(a q e) f -> a q e f", q=P, e=PAIR)[a],
            )
            nc.sync.dma_start(out=z_all[:, FIRST_TILES + a, :], in_=z_tiles[:, FIRST_TILES + a, :])
        for i in range(FIRST_TILES + HID_BLOCKS // PAIR, ROW_TILES):
            nc.sync.dma_start(out=z_all[:, i, :], in_=z_tiles[:, i, :])
        nc.sync.dma_start(
            out=w2_raw[:].rearrange("q (a e) h -> q a e h", e=PAIR),
            in_=se_w2.rearrange("(a q e) h -> q a e h", q=P, e=PAIR),
        )

        vec_rows = keep.tile([P, PAIR * P], BF16)
        nc.vector.memset(vec_rows[:], 0.0)
        for first_col, vec in ((GAMMA, ln_gamma), (BETA, ln_beta), (B2, se_b2), (B1, se_b1)):
            rows_of_vec = vec.rearrange("(a w) -> a w", w=PAIR * P)
            first_row = first_col // PAIR
            nc.scalar.dma_start(out=vec_rows[first_row : first_row + rows_of_vec.shape[0], :], in_=rows_of_vec)

        minus_half = keep.tile([P, ROUND_TILES], F32)
        nc.gpsimd.memset(minus_half[:], -0.5)
        ident = keep.tile([P, P], F32)
        make_identity(nc, ident[:])
        table_warmer = keep.tile([P, 1], F32)
        nc.scalar.activation(out=table_warmer[:], in_=minus_half[:, 0:1], func=ACT.Sigmoid)

        vec_cols = keep.tile([P, VEC_COLS], F32)

        def flip_vectors():
            vec_flip = flip.tile([P, P], F32, tag="flip")
            nc.tensor.transpose(vec_flip[:], vec_rows[:].bitcast(F32), ident[:])
            nc.scalar.copy(out=vec_cols[:], in_=vec_flip[:].bitcast(BF16)[:, 0:VEC_COLS])

        w_grouped = keep.tile([P, LAYERS * LAYER_WORDS * PACK], BF16, align_bytes=64)
        w_codes = keep.tile([P, LAYERS * LAYER_WORDS], U32, align_bytes=64)
        w_scales = keep.tile([P, LAYERS * LAYER_WORDS], U8, align_bytes=64)
        y_t = keep.tile([P, FEAT_BLOCKS, ROWS], F32)
        y_grouped = keep.tile([P, ROUNDS, FEAT_PASSES, ROUND_ROWS, PACK], BF16, align_bytes=64)
        y_codes = keep.tile([P, ROUNDS, FEAT_PASSES, ROUND_ROWS], U32, align_bytes=64)
        y_scales = keep.tile([P, ROUNDS, FEAT_PASSES, ROUND_ROWS], U8, align_bytes=64)
        h_planes = keep.tile([P, HID_BLOCKS, ROWS], BF16)
        h_grouped = keep.tile([P, ROWS, PACK], BF16, align_bytes=64)
        h_codes = keep.tile([P, ROWS], U32, align_bytes=64)
        h_scales = keep.tile([P, ROWS], U8, align_bytes=64)
        gate_t = keep.tile([P, FEAT_BLOCKS, ROWS], F32)
        stats = keep.tile([P, ROW_TILES, FEAT_BANKS, 6], F32)
        mean_var = keep.tile([P, ROW_TILES, 2], F32)
        var_eps = keep.tile([P, ROW_TILES], F32)
        rstd = keep.tile([P, ROW_TILES], F32)
        shift = keep.tile([P, ROW_TILES], F32)

        w_grouped_words = w_grouped[:].bitcast(F32).rearrange("p (r u) -> p r u", u=PAIR)
        w1_words = w1_raw[:].rearrange("q m f -> q (m f)").bitcast(F32).rearrange("q (m w) -> q m w", m=HID_BLOCKS)
        w2_words = w2_raw[:].rearrange("q j h -> q (j h)").bitcast(F32).rearrange("q (j w) -> q j w", j=FEAT_BLOCKS)
        PASS_WORDS = K_PASS // PAIR

        def stationary_blocks(layer):
            if layer == 0:
                return [
                    w1_words[:, m, c * PASS_WORDS : (c + 1) * PASS_WORDS]
                    for c in range(FEAT_PASSES)
                    for m in range(HID_BLOCKS)
                ]
            return [w2_words[:, j, :] for j in range(FEAT_BLOCKS)]

        def flip_layer(layer):
            blocks = stationary_blocks(layer)
            pairs = range(0, len(blocks), PAIR)
            if layer == 0:
                pairs = sorted(pairs, key=lambda first: first % HID_BLOCKS)
            for first in pairs:
                flipped = flip.tile([P, PAIR, PAIR, P], F32, tag="flip")
                for b in range(PAIR):
                    for u in range(PAIR):
                        nc.tensor.transpose(flipped[:, b, u, :], blocks[first + b][:, u * P : (u + 1) * P], ident[:])
                words = slice(layer * LAYER_WORDS + first * P, layer * LAYER_WORDS + (first + PAIR) * P)
                nc.scalar.copy(
                    out=w_grouped_words[:, words, :].rearrange("p (b r) u -> p b r u", b=PAIR),
                    in_=flipped[:].rearrange("p b u r -> p b r u"),
                )

        def quantise_layer(layer):
            words = slice(layer * LAYER_WORDS, (layer + 1) * LAYER_WORDS)
            nc.vector.quantize_mx(
                out=w_codes[:, words].bitcast(FP8X4),
                scales=w_scales[:, words],
                in_=w_grouped[:, layer * LAYER_WORDS * PACK : (layer + 1) * LAYER_WORDS * PACK],
            )

        def tiles_of(n):
            return range(n * ROUND_TILES, (n + 1) * ROUND_TILES)

        def rows_of(n):
            return slice(n * ROUND_ROWS, (n + 1) * ROUND_ROWS)

        def statistics(i):
            for b in range(FEAT_BANKS):
                nc.vector.bn_stats(out=stats[:, i, b, :], in_=z_all[:, i, b * BANK : (b + 1) * BANK])

        def aggregate(i):
            nc.vector.bn_aggr(out=mean_var[:, i, :], in_=stats[:, i, :, :].rearrange("p b d -> p (b d)"))

        def reciprocal_deviation(n):
            tiles = slice(n * ROUND_TILES, (n + 1) * ROUND_TILES)
            nc.gpsimd.tensor_scalar(
                out=var_eps[:, tiles],
                in0=mean_var[:, tiles, 1],
                scalar1=1.0,
                scalar2=LN_EPS,
                op0=ALU.mult,
                op1=ALU.add,
            )
            nc.gpsimd.tensor_tensor(out=rstd[:, tiles], in0=var_eps[:, tiles], in1=minus_half[:], op=ALU.pow)

        def shifts(n):
            for i in tiles_of(n):
                if i in SCALAR_TILES + GPSIMD_TILES:
                    col = slice(i, i + 1)
                    nc.gpsimd.tensor_scalar(
                        out=shift[:, col],
                        in0=mean_var[:, i, 0:1],
                        scalar1=-1.0,
                        scalar2=rstd[:, col],
                        op0=ALU.mult,
                        op1=ALU.mult,
                    )

        def normalise(i):
            xhat = work.tile([P, FEAT_BLOCKS, P], F32)
            xhats[i] = xhat
            sorted_out = xhat[:].rearrange("p (a e) q -> p a e q", e=PAIR)
            z_in = z_all[:, i, :].rearrange("p (a q e) -> p a e q", q=P, e=PAIR)
            if i in GPSIMD_TILES:
                nc.gpsimd.tensor_scalar(
                    out=sorted_out,
                    in0=z_in,
                    scalar1=rstd[:, i : i + 1],
                    scalar2=shift[:, i : i + 1],
                    op0=ALU.mult,
                    op1=ALU.add,
                )
            elif i in SCALAR_TILES:
                nc.scalar.activation(
                    out=sorted_out,
                    in_=z_in,
                    func=ACT.Identity,
                    scale=rstd[:, i : i + 1],
                    bias=shift[:, i : i + 1],
                )
            else:
                nc.vector.tensor_scalar(
                    out=sorted_out,
                    in0=z_in,
                    scalar1=mean_var[:, i, 0:1],
                    scalar2=rstd[:, i : i + 1],
                    op0=ALU.subtract,
                    op1=ALU.mult,
                )

        def affine(n):
            for first in range(0, FEAT_BLOCKS, PER_BANK):
                flipped = flip.tile([P, PER_BANK, ROUND_ROWS], F32, tag="flip")
                for g in range(PER_BANK):
                    for a, i in enumerate(tiles_of(n)):
                        nc.tensor.transpose(flipped[:, g, a * P : (a + 1) * P], xhats[i][:, first + g, :], ident[:])
                for g in range(PER_BANK):
                    j = first + g
                    nc.scalar.activation(
                        out=y_t[:, j, rows_of(n)],
                        in_=flipped[:, g, :],
                        func=ACT.Identity,
                        scale=vec_cols[:, GAMMA + j : GAMMA + j + 1],
                        bias=vec_cols[:, BETA + j : BETA + j + 1],
                    )

        def regroup_y(n):
            nc.vector.tensor_copy(
                out=y_grouped[:, n].rearrange("p c (q i) t -> p c q t i", i=RUN),
                in_=y_t[:, :, rows_of(n)].rearrange("p (c t) (q i) -> p c q t i", t=PACK, i=RUN),
            )

        def quantise_y(n):
            nc.vector.quantize_mx(
                out=y_codes[:, n].rearrange("p c r -> p (c r)").bitcast(FP8X4),
                scales=y_scales[:, n].rearrange("p c r -> p (c r)"),
                in_=y_grouped[:, n].rearrange("p c r t -> p (c r t)"),
            )

        def hidden_layer(n):
            for first in range(0, HID_BLOCKS, PER_BANK):
                h_sum = sums.tile([P, PER_BANK, ROUND_ROWS], F32, tag="sums")
                for g in range(PER_BANK):
                    for c in range(FEAT_PASSES):
                        units = slice((c * HID_BLOCKS + first + g) * P, (c * HID_BLOCKS + first + g + 1) * P)
                        nc.tensor.matmul_mx(
                            out=h_sum[:, g, :],
                            lhsT=w_codes[:, units].bitcast(FP8X4),
                            lhsT_scale=w_scales[:, units],
                            rhs=y_codes[:, n, c, :].bitcast(FP8X4),
                            rhs_scale=y_scales[:, n, c, :],
                            start=(c == 0),
                            stop=(c == FEAT_PASSES - 1),
                        )
                for g in range(PER_BANK):
                    m = first + g
                    nc.scalar.activation(
                        out=h_planes[:, m, rows_of(n)],
                        in_=h_sum[:, g, :],
                        func=ACT.Relu,
                        bias=vec_cols[:, B1 + m : B1 + m + 1],
                    )

        def regroup_h(n):
            nc.vector.tensor_copy(
                out=h_grouped[:, rows_of(n), :].rearrange("p (q i) m -> p q m i", i=RUN),
                in_=h_planes[:, :, rows_of(n)].rearrange("p m (q i) -> p q m i", i=RUN),
            )

        def quantise_h(n):
            nc.vector.quantize_mx(
                out=h_codes[:, rows_of(n)].bitcast(FP8X4),
                scales=h_scales[:, rows_of(n)],
                in_=h_grouped[:, rows_of(n), :].rearrange("p r m -> p (r m)"),
            )

        def gate_layer(n):
            for first in range(0, FEAT_BLOCKS, PER_BANK):
                g_sum = sums.tile([P, PER_BANK, ROUND_ROWS], F32, tag="sums")
                for g in range(PER_BANK):
                    feats = slice(LAYER_WORDS + (first + g) * P, LAYER_WORDS + (first + g + 1) * P)
                    nc.tensor.matmul_mx(
                        out=g_sum[:, g, :],
                        lhsT=w_codes[:, feats].bitcast(FP8X4),
                        lhsT_scale=w_scales[:, feats],
                        rhs=h_codes[:, rows_of(n)].bitcast(FP8X4),
                        rhs_scale=h_scales[:, rows_of(n)],
                        start=True,
                        stop=True,
                    )
                for g in range(PER_BANK):
                    j = first + g
                    nc.scalar.activation(
                        out=gate_t[:, j, rows_of(n)],
                        in_=g_sum[:, g, :],
                        func=ACT.Sigmoid,
                        bias=vec_cols[:, B2 + j : B2 + j + 1],
                    )

        def products(n):
            for b in range(FEAT_BANKS):
                blocks = slice(b * PACK, (b + 1) * PACK)
                nc.vector.tensor_tensor(
                    out=gate_t[:, blocks, rows_of(n)],
                    in0=gate_t[:, blocks, rows_of(n)],
                    in1=y_t[:, blocks, rows_of(n)],
                    op=ALU.mult,
                )

        def flip_back(i, b):
            rows = slice(i * P, (i + 1) * P)
            back = flip.tile([P, PACK, P], F32, tag="flip")
            for g in range(PACK):
                nc.tensor.transpose(back[:, g, :], gate_t[:, b * PACK + g, rows], ident[:])
            return back

        def store(i, b, back, copy):
            result = work.tile([P, BANK], F32, bufs=RESULT_TILES)
            copy(
                out=result[:].rearrange("p (a q e) -> p a q e", q=P, e=PAIR),
                in_=back[:].rearrange("p (a e) q -> p a q e", e=PAIR),
            )
            nc.sync.dma_start(out=out[i * P : (i + 1) * P, b * BANK : (b + 1) * BANK], in_=result[:])

        def vector_store():
            for i, b, back in left_over:
                store(i, b, back, nc.vector.tensor_copy)
            left_over.clear()

        def stores(n, b):
            vector_store()
            for i in tiles_of(n):
                back = flip_back(i, b)
                if i % ROUND_TILES == 1 and (n, b) != (2, 0):
                    left_over.append((i, b, back))
                else:
                    store(i, b, back, nc.scalar.copy)

        xhats = {}
        left_over = []
        flip_layer(0)
        flip_vectors()
        for n in range(-1, ROUNDS + LAG_PRODUCT + 1):
            y_round, h_round, done = n - LAG_HIDDEN, n - LAG_GATE, n - LAG_PRODUCT
            ahead = list(tiles_of(n + 1)) if n + 1 < ROUNDS else []
            own = [i for i in tiles_of(n) if i not in SCALAR_TILES + GPSIMD_TILES] if 0 <= n < ROUNDS else []
            order = [(statistics, i) for i in ahead] + [(normalise, i) for i in own]
            if n == 0:
                order[1], order[2] = order[2], order[1]
            for stage, i in order:
                stage(i)
            if n + 1 < ROUNDS:
                for i in tiles_of(n + 1):
                    aggregate(i)
                reciprocal_deviation(n + 1)
                shifts(n + 1)
                for i in tiles_of(n + 1):
                    if i in GPSIMD_TILES:
                        normalise(i)
            if 0 <= n < ROUNDS:
                for i in tiles_of(n):
                    if i in SCALAR_TILES:
                        normalise(i)
                affine(n)
            if n == 0:
                flip_layer(1)
            if n == LAG_HIDDEN:
                quantise_layer(0)
            if 0 <= y_round < ROUNDS:
                regroup_y(y_round)
            if 0 <= h_round < ROUNDS:
                regroup_h(h_round)
            if 0 <= y_round < ROUNDS:
                quantise_y(y_round)
                hidden_layer(y_round)
            if n == LAG_GATE:
                quantise_layer(1)
            if 0 <= done - 1 < ROUNDS:
                stores(done - 1, 1)
            if 0 <= h_round < ROUNDS:
                quantise_h(h_round)
                gate_layer(h_round)
            if 0 <= done < ROUNDS:
                products(done)
                stores(done, 0)
        vector_store()
